import numpy as np
import ml_dtypes


def mxq(x, axis, fmt="e4m3"):
    dtype, down = {"e4m3": (ml_dtypes.float8_e4m3fn, 7), "e5m2": (ml_dtypes.float8_e5m2, 14)}[fmt]
    v = np.moveaxis(np.asarray(x, np.float32).astype(ml_dtypes.bfloat16).astype(np.float64), axis, -1)
    blocks = v.reshape(v.shape[:-1] + (-1, 32))
    amax = np.abs(blocks).max(-1, keepdims=True)
    byte = np.maximum(np.where(amax > 0, np.frexp(amax)[1] - 1 + 127, 0) - down, 1)
    scale = np.exp2(byte - 127.0)
    codes = (blocks / scale).astype(np.float32).astype(dtype).astype(np.float64)
    return np.moveaxis((codes * scale).reshape(v.shape), -1, axis)


WIDE = False


def mx_kscale(k):
    if not WIDE:
        return np.ones(k)
    levels = np.array([10, -10, 5, -5, 0])
    if k % 512:
        return np.exp2(np.random.permutation(np.resize(levels, k // 32))).repeat(32)
    a = np.empty((k // 512, 16))
    for p in range(k // 512):
        a[p, :8] = np.random.permutation(np.resize(levels, 8))
        for g in range(8):
            far = levels[np.abs(levels - a[p, g]) >= 10]
            a[p, g + 8] = far[np.random.randint(len(far))]
    return np.exp2(a.ravel()).repeat(32)


BF16 = ml_dtypes.bfloat16


def bf(x):
    return np.asarray(x, np.float32).astype(BF16)


def f64(x):
    return np.asarray(x).astype(np.float64)


B, N, DIM, H, HKV, D, CACHE, WINDOW = 1, 512, 2048, 16, 4, 128, 1536, 1024
EPS = 1e-6
THETA = 10000.0
HALF = D // 2


def rms_norm(t, w):
    return t * (1.0 / np.sqrt(np.mean(t * t, axis=-1, keepdims=True) + EPS)) * w


def rope(t, cos, sin):
    t2 = t.reshape(*t.shape[:-1], HALF, 2)
    x0, x1 = t2[..., 0], t2[..., 1]
    c = cos[None, None, :, :]
    s = sin[None, None, :, :]
    r0 = x0 * c - x1 * s
    r1 = x0 * s + x1 * c
    return np.stack([r0, r1], axis=-1).reshape(t.shape)


def setup_inputs():
    s = mx_kscale(DIM)
    ang = np.arange(CACHE, CACHE + N)[:, None] * (1.0 / THETA ** (np.arange(0, D, 2) / D))[None, :]
    return {"x": bf(np.random.standard_normal((B, N, DIM)) * s),
            "freqs_cos": bf(np.cos(ang)), "freqs_sin": bf(np.sin(ang)),
            "Wq": bf(np.random.standard_normal((H * D, DIM)) / np.sqrt(DIM) / s[None, :]),
            "Wk": bf(np.random.standard_normal((HKV * D, DIM)) / np.sqrt(DIM) / s[None, :]),
            "Wv": bf(np.random.standard_normal((HKV * D, DIM)) / np.sqrt(DIM) / s[None, :]),
            "wq_norm": bf(2.0 + 0.2 * np.random.standard_normal(D)),
            "wk_norm": bf(1.0 + 0.1 * np.random.standard_normal(D))}


def reference(x, freqs_cos, freqs_sin, Wq, Wk, Wv, wq_norm, wk_norm):
    xq = mxq(f64(x), 2, "e4m3")
    q = (xq @ mxq(f64(Wq), 1, "e4m3").T).reshape(B, N, H, D).transpose(0, 2, 1, 3)
    k = (xq @ mxq(f64(Wk), 1, "e4m3").T).reshape(B, N, HKV, D).transpose(0, 2, 1, 3)
    v = (xq @ mxq(f64(Wv), 1, "e4m3").T).reshape(B, N, HKV, D).transpose(0, 2, 1, 3)
    q = rms_norm(q, f64(wq_norm))
    k = rms_norm(k, f64(wk_norm))
    q = rope(q, f64(freqs_cos), f64(freqs_sin))
    k = rope(k, f64(freqs_cos), f64(freqs_sin))
    return q, k, v

@@ -1,0 +1,299 @@
+from contextlib import ExitStack
+
+import concourse.masks as masks
+import concourse.mybir as mybir
+
+F32 = mybir.dt.float32
+BF16 = mybir.dt.bfloat16
+U32 = mybir.dt.uint32
+U8 = mybir.dt.uint8
+FP8X4 = mybir.dt.float8_e4m3fn_x4
+ACT = mybir.ActivationFunctionType
+ALU = mybir.AluOpType
+
+P = 128
+TOKENS = 512
+TOKEN_TILES = TOKENS // P
+K = 2048
+K_PASS = 4 * P
+PASSES = K // K_PASS
+HEAD = 128
+HALF = HEAD // 2
+ROWS = 2 * P
+EPS = 1e-6
+
+Q_PAIRS, K_PAIRS, V_PAIRS = 8, 2, 2
+PAIRS = Q_PAIRS + K_PAIRS + V_PAIRS
+OPERANDS = 2 + PAIRS
+FLIP_STEPS = 2 * OPERANDS
+SLOTS = 2 * PAIRS
+MULTIPLY_LAG = 7
+PRODUCTS_LAG = MULTIPLY_LAG + 1
+FINISH_LAG = MULTIPLY_LAG + 3
+STEPS = SLOTS + MULTIPLY_LAG
+
+FLOPS = 2 * TOKENS * K * HEAD * 2 * PAIRS
+
+
+def tile_slidingcacheattention_pa_kernel(
+    tc, x, freqs_cos, freqs_sin, Wq, Wk, Wv, wq_norm, wk_norm, out_0, out_1, out_2
+):
+    nc = tc.nc
+    with ExitStack() as stack:
+        stack.enter_context(tc.manual_schedule())
+        const = stack.enter_context(tc.tile_pool(name="const", bufs=1))
+        rows_pool = stack.enter_context(tc.tile_pool(name="rows", bufs=OPERANDS))
+        stage = stack.enter_context(tc.tile_pool(name="stage", bufs=3))
+        w_mx = stack.enter_context(tc.tile_pool(name="w_mx", bufs=4))
+        work = stack.enter_context(tc.tile_pool(name="work", bufs=3))
+        flip_psum = stack.enter_context(tc.psum_pool(name="flip_psum", bufs=4))
+        acc_psum = stack.enter_context(tc.psum_pool(name="acc_psum", bufs=4))
+
+        cos = const.tile([P, TOKEN_TILES, HALF], BF16)
+        sin = const.tile([P, TOKEN_TILES, HALF], BF16)
+        gain_rows = const.tile([P, 2 * HEAD], BF16)
+        nc.vector.memset(gain_rows[:], 0.0)
+        nc.sync.dma_start(out=gain_rows[0:1, 0:HEAD], in_=wq_norm.rearrange("(o d) -> o d", o=1))
+        nc.sync.dma_start(out=gain_rows[0:1, HEAD : 2 * HEAD], in_=wk_norm.rearrange("(o d) -> o d", o=1))
+        nc.sync.dma_start(out=cos[:], in_=freqs_cos.rearrange("(p j) i -> p j i", j=TOKEN_TILES))
+        nc.sync.dma_start(out=sin[:], in_=freqs_sin.rearrange("(p j) i -> p j i", j=TOKEN_TILES))
+
+        x_view = x[0].rearrange("(p j) k -> p j k", j=TOKEN_TILES)
+        pairs = [("q", Wq, out_0, n) for n in range(Q_PAIRS)]
+        pairs.extend([("k", Wk, out_1, n) for n in range(K_PAIRS)])
+        pairs.extend([("v", Wv, out_2, n) for n in range(V_PAIRS)])
+        pair_views = [w[ROWS * n : ROWS * (n + 1), :].rearrange("(b p) k -> p b k", p=P) for (kind, w, out, n) in pairs]
+        operands = [("x", x_view[:, 0:2, :]), (pairs[0][0], pair_views[0]), ("x", x_view[:, 2:4, :])]
+        operands.extend([(pairs[w][0], pair_views[w]) for w in range(1, PAIRS)])
+        rows = []
+        for kind, view in operands:
+            loaded = rows_pool.tile([P, 2 * K], BF16)
+            nc.sync.dma_start(out=loaded[:].rearrange("p (b k) -> p b k", b=2), in_=view)
+            rows.append(loaded)
+
+        eps = const.tile([P, 1], F32)
+        nc.vector.memset(eps[:], EPS)
+        warm = const.tile([P, 1], F32)
+        nc.scalar.activation(out=warm[:], in_=eps[:], func=ACT.Sqrt)
+
+        ident = const.tile([P, P], F32)
+        masks.make_identity(nc, ident[:])
+        evens_first = const.tile([P, P], F32)
+        nc.vector.tensor_copy(
+            out=evens_first[:].rearrange("p (e i) -> p e i", e=2),
+            in_=ident[:].rearrange("p (i e) -> p e i", e=2),
+        )
+
+        ones = const.tile([P, P], BF16)
+        nc.vector.memset(ones[:], 1.0)
+        gain_psum = flip_psum.tile([P, 2 * HEAD], F32, tag="flipped")
+        nc.tensor.matmul(out=gain_psum[:], lhsT=ones[:], rhs=gain_rows[:], start=True, stop=True)
+        gains = const.tile([P, 2 * HEAD], F32)
+        minus_gains = const.tile([P, 2 * HEAD], F32)
+        nc.vector.tensor_copy(out=gains[:], in_=gain_psum[:])
+        nc.vector.tensor_scalar_mul(out=minus_gains[:], in0=gain_psum[:], scalar1=-1.0)
+
+        tables = {}
+        for n, kind in enumerate(("q", "k")):
+
+            def every_second(vector, e):
+                halves = vector[:, HEAD * n : HEAD * (n + 1)].rearrange("p (i e) -> p e i", e=2)
+                return halves[:, e, :].unsqueeze(1).to_broadcast([P, TOKEN_TILES, HALF])
+
+            same = const.tile([P, TOKEN_TILES, 2, HALF], F32, name="same_" + kind)
+            cross = const.tile([P, TOKEN_TILES, 2, HALF], F32, name="cross_" + kind)
+            nc.gpsimd.tensor_tensor(out=same[:, :, 0, :], in0=cos[:], in1=every_second(gains, 0), op=ALU.mult)
+            nc.gpsimd.tensor_tensor(out=same[:, :, 1, :], in0=cos[:], in1=every_second(gains, 1), op=ALU.mult)
+            nc.gpsimd.tensor_tensor(out=cross[:, :, 0, :], in0=sin[:], in1=every_second(minus_gains, 1), op=ALU.mult)
+            nc.gpsimd.tensor_tensor(out=cross[:, :, 1, :], in0=sin[:], in1=every_second(gains, 0), op=ALU.mult)
+            tables[kind] = (same, cross)
+
+        flipped = {}
+        grouped = {}
+        codes = {}
+        scales = {}
+        acc = {}
+        stats = {}
+        own = {}
+        partner = {}
+        result = {}
+
+        def flip(step):
+            kind = operands[step // 2][0]
+            order = ident if kind in ("x", "v") else evens_first
+            words = rows[step // 2][:].bitcast(F32)
+            flipped[step] = []
+            for g in (2 * (step % 2), 2 * (step % 2) + 1):
+                bank = flip_psum.tile([P, 2, 2, P], F32, name="flipped")
+                for b in range(2):
+                    for u in range(2):
+                        first = b * (K // 2) + g * (K_PASS // 2)
+                        nc.tensor.transpose(
+                            bank[:, b, u, :], words[:, first + u : first + K_PASS // 2 : 2], order[:]
+                        )
+                flipped[step].append(bank)
+
+        def regroup(step):
+            grouped[step] = stage.tile([P, 2, 4 * ROWS], BF16, name="grouped", align_bytes=64)
+            for half, bank in enumerate(flipped[step]):
+                out_words = grouped[step][:, half, :].bitcast(F32).rearrange("p (b r u) -> p b r u", b=2, u=2)
+                in_words = bank[:].rearrange("p b u r -> p b r u")
+                if step % 2 == 1 and half == 1:
+                    nc.vector.tensor_copy(out=out_words, in_=in_words)
+                else:
+                    nc.scalar.copy(out=out_words, in_=in_words)
+
+        def quantise(step):
+            tile_index = step // 2
+            if step % 2 == 0:
+                if operands[tile_index][0] == "x":
+                    codes[tile_index] = const.tile([P, PASSES, ROWS], U32, name="x_codes%d" % tile_index, align_bytes=64)
+                    scales[tile_index] = const.tile([P, PASSES, ROWS], U8, name="x_scales%d" % tile_index, align_bytes=64)
+                else:
+                    codes[tile_index] = w_mx.tile([P, PASSES, ROWS], U32, name="w_codes", align_bytes=64)
+                    scales[tile_index] = w_mx.tile([P, PASSES, ROWS], U8, name="w_scales", align_bytes=64)
+            two_passes = slice(2 * (step % 2), 2 * (step % 2) + 2)
+            nc.vector.quantize_mx(
+                out=codes[tile_index][:, two_passes, :].rearrange("p g r -> p (g r)").bitcast(FP8X4),
+                scales=scales[tile_index][:, two_passes, :].rearrange("p g r -> p (g r)"),
+                in_=grouped[step][:].rearrange("p g c -> p (g c)"),
+            )
+
+        def multiply(slot):
+            pair, half = slot // 2, slot % 2
+            x_tile = 2 * half
+            w_tile = 1 if pair == 0 else pair + 2
+            acc[slot] = acc_psum.tile([P, 2, 2 * HEAD], F32, name="acc")
+            for jj in range(2):
+                tok = slice(P * jj, P * (jj + 1))
+                for g in range(PASSES):
+                    nc.tensor.matmul_mx(
+                        out=acc[slot][:, jj, :],
+                        lhsT=codes[x_tile][:, g, tok].bitcast(FP8X4),
+                        lhsT_scale=scales[x_tile][:, g, tok],
+                        rhs=codes[w_tile][:, g, :].bitcast(FP8X4),
+                        rhs_scale=scales[w_tile][:, g, :],
+                        start=(g == 0),
+                        stop=(g == PASSES - 1),
+                    )
+
+        def segments(slot):
+            half = slot % 2
+            return [
+                (acc[slot][:, jj, HEAD * hh : HEAD * (hh + 1)], 4 * half + 2 * jj + hh, TOKEN_TILES * hh + 2 * half + jj)
+                for jj in range(2)
+                for hh in range(2)
+            ]
+
+        def squares(slot):
+            pair, half = slot // 2, slot % 2
+            if half == 0:
+                stats[pair] = [work.tile([P, 8], F32, name=name) for name in ("sumsq", "rms", "inv_rms")]
+            sumsq, rms, inv_rms = stats[pair]
+            for segment, column, row in segments(slot):
+                scratch = work.tile([P, HEAD], F32, name="scratch")
+                nc.scalar.activation(
+                    out=scratch[:], in_=segment, func=ACT.Square, accum_out=sumsq[:, column : column + 1]
+                )
+            these = slice(4 * half, 4 * half + 4)
+            nc.scalar.activation(out=rms[:, these], in_=sumsq[:, these], func=ACT.Sqrt, bias=eps[:], scale=1.0 / HEAD)
+
+        def invert(slot):
+            sumsq, rms, inv_rms = stats[slot // 2]
+            these = slice(4 * (slot % 2), 4 * (slot % 2) + 4)
+            nc.vector.reciprocal(out=inv_rms[:, these], in_=rms[:, these])
+
+        def slot_rows(tile_of_pair, half):
+            return tile_of_pair[:].rearrange("p (h j) d -> p j h d", h=2)[:, 2 * half : 2 * half + 2, :, :]
+
+        def products(slot):
+            pair, half = slot // 2, slot % 2
+            if half == 0:
+                own[pair] = work.tile([P, 2 * TOKEN_TILES, HEAD], F32, name="own")
+                partner[pair] = work.tile([P, 2 * TOKEN_TILES, HEAD], F32, name="partner")
+            same, cross = tables[pairs[pair][0]]
+            tiles = slice(2 * half, 2 * half + 2)
+            sums = acc[slot][:].rearrange("p j (h d) -> p j h d", h=2)
+            nc.vector.tensor_tensor(
+                out=slot_rows(own[pair], half),
+                in0=sums,
+                in1=same[:, tiles, :, :].rearrange("p j e i -> p j (e i)").unsqueeze(2).to_broadcast([P, 2, 2, HEAD]),
+                op=ALU.mult,
+            )
+            for e in range(2):
+                mine = slice(HALF * e, HALF * (e + 1))
+                other = slice(HALF * (1 - e), HALF * (2 - e))
+                nc.vector.tensor_tensor(
+                    out=slot_rows(partner[pair], half)[:, :, :, mine],
+                    in0=sums[:, :, :, other],
+                    in1=cross[:, tiles, e, :].unsqueeze(2).to_broadcast([P, 2, 2, HALF]),
+                    op=ALU.mult,
+                )
+
+        def add(slot):
+            pair, half = slot // 2, slot % 2
+            nc.gpsimd.tensor_tensor(
+                out=slot_rows(own[pair], half),
+                in0=slot_rows(own[pair], half),
+                in1=slot_rows(partner[pair], half),
+                op=ALU.add,
+            )
+
+        def finish(slot):
+            pair = slot // 2
+            if slot % 2 == 0:
+                result[pair] = work.tile([P, 2 * TOKEN_TILES, HEAD], F32, name="result")
+            inv_rms = stats[pair][2]
+            for segment, column, row in segments(slot):
+                nc.scalar.activation(
+                    out=result[pair][:, row, :].rearrange("p (i e) -> p i e", e=2),
+                    in_=own[pair][:, row, :].rearrange("p (e i) -> p i e", e=2),
+                    func=ACT.Copy,
+                    scale=inv_rms[:, column : column + 1],
+                )
+
+        def copy_v(slot):
+            pair, half = slot // 2, slot % 2
+            if half == 0:
+                result[pair] = work.tile([P, 2 * TOKEN_TILES, HEAD], F32, name="result")
+            out_view = result[pair][:].rearrange("p (h j) d -> p j h d", h=2)[:, 2 * half : 2 * half + 2, :, :]
+            in_view = acc[slot][:].rearrange("p j (h d) -> p j h d", h=2)
+            if half == 0:
+                nc.scalar.copy(out=out_view, in_=in_view)
+            else:
+                nc.vector.tensor_copy(out=out_view, in_=in_view)
+
+        def store(pair):
+            kind, w, out, n = pairs[pair]
+            nc.sync.dma_start(
+                out=out[0, 2 * n : 2 * n + 2].rearrange("h (p j) d -> p h (j d)", j=TOKEN_TILES),
+                in_=result[pair][:].rearrange("p (h j) d -> p h (j d)", h=2),
+            )
+
+        def rotated(slot):
+            return 0 <= slot < SLOTS and pairs[slot // 2][0] != "v"
+
+        for step in range(STEPS):
+            if step < FLIP_STEPS:
+                flip(step)
+            if rotated(step - PRODUCTS_LAG):
+                invert(step - PRODUCTS_LAG)
+                products(step - PRODUCTS_LAG)
+                add(step - PRODUCTS_LAG)
+            if 0 <= step - 1 < FLIP_STEPS:
+                quantise(step - 1)
+            if step < FLIP_STEPS:
+                regroup(step)
+            slot = step - MULTIPLY_LAG
+            if slot >= 0:
+                multiply(slot)
+            if rotated(step - FINISH_LAG):
+                finish(step - FINISH_LAG)
+                if (step - FINISH_LAG) % 2 == 1:
+                    store((step - FINISH_LAG) // 2)
+            if rotated(slot):
+                squares(slot)
+            elif slot >= 0:
+                copy_v(slot)
+                if slot % 2 == 1:
+                    store(slot // 2)

@@ -17,6 +17,7 @@ TOKEN_TILES = TOKENS // P
 K = 2048
 K_PASS = 4 * P
 PASSES = K // K_PASS
+WORDS = K // 2
 HEAD = 128
 HALF = HEAD // 2
 ROWS = 2 * P
@@ -25,12 +26,12 @@ EPS = 1e-6
 Q_PAIRS, K_PAIRS, V_PAIRS = 8, 2, 2
 PAIRS = Q_PAIRS + K_PAIRS + V_PAIRS
 OPERANDS = 2 + PAIRS
-FLIP_STEPS = 2 * OPERANDS
-SLOTS = 2 * PAIRS
-MULTIPLY_LAG = 7
-PRODUCTS_LAG = MULTIPLY_LAG + 1
-FINISH_LAG = MULTIPLY_LAG + 3
-STEPS = SLOTS + MULTIPLY_LAG
+X_TILES = (0, 2)
+
+
+def w_tile(pair):
+    return 1 if pair == 0 else pair + 2
+
 
 FLOPS = 2 * TOKENS * K * HEAD * 2 * PAIRS
 
@@ -43,9 +44,9 @@ def tile_slidingcacheattention_pa_kernel(
         stack.enter_context(tc.manual_schedule())
         const = stack.enter_context(tc.tile_pool(name="const", bufs=1))
         rows_pool = stack.enter_context(tc.tile_pool(name="rows", bufs=OPERANDS))
-        stage = stack.enter_context(tc.tile_pool(name="stage", bufs=3))
-        w_mx = stack.enter_context(tc.tile_pool(name="w_mx", bufs=4))
-        work = stack.enter_context(tc.tile_pool(name="work", bufs=3))
+        stage = stack.enter_context(tc.tile_pool(name="stage", bufs=2))
+        w_mx = stack.enter_context(tc.tile_pool(name="w_mx", bufs=3))
+        work = stack.enter_context(tc.tile_pool(name="work", bufs=4))
         flip_psum = stack.enter_context(tc.psum_pool(name="flip_psum", bufs=4))
         acc_psum = stack.enter_context(tc.psum_pool(name="acc_psum", bufs=4))
 
@@ -63,116 +64,111 @@ def tile_slidingcacheattention_pa_kernel(
         pairs.extend([("k", Wk, out_1, n) for n in range(K_PAIRS)])
         pairs.extend([("v", Wv, out_2, n) for n in range(V_PAIRS)])
         pair_views = [w[ROWS * n : ROWS * (n + 1), :].rearrange("(b p) k -> p b k", p=P) for (kind, w, out, n) in pairs]
-        operands = [("x", x_view[:, 0:2, :]), (pairs[0][0], pair_views[0]), ("x", x_view[:, 2:4, :])]
-        operands.extend([(pairs[w][0], pair_views[w]) for w in range(1, PAIRS)])
+        views = [x_view[:, 0:2, :], pair_views[0], x_view[:, 2:4, :]]
+        views.extend(pair_views[1:])
         rows = []
-        for kind, view in operands:
-            loaded = rows_pool.tile([P, 2 * K], BF16)
-            nc.sync.dma_start(out=loaded[:].rearrange("p (b k) -> p b k", b=2), in_=view)
+        for view in views:
+            loaded = rows_pool.tile([P, 2, K], BF16, name="loaded")
+            nc.sync.dma_start(out=loaded[:], in_=view)
             rows.append(loaded)
 
         eps = const.tile([P, 1], F32)
         nc.vector.memset(eps[:], EPS)
         warm = const.tile([P, 1], F32)
-        nc.scalar.activation(out=warm[:], in_=eps[:], func=ACT.Sqrt)
+        nc.scalar.activation(out=warm[:], in_=eps[:], func=ACT.Abs_reciprocal_sqrt)
 
         ident = const.tile([P, P], F32)
         masks.make_identity(nc, ident[:])
-        evens_first = const.tile([P, P], F32)
-        nc.vector.tensor_copy(
-            out=evens_first[:].rearrange("p (e i) -> p e i", e=2),
-            in_=ident[:].rearrange("p (i e) -> p e i", e=2),
-        )
 
         ones = const.tile([P, P], BF16)
         nc.vector.memset(ones[:], 1.0)
         gain_psum = flip_psum.tile([P, 2 * HEAD], F32, tag="flipped")
         nc.tensor.matmul(out=gain_psum[:], lhsT=ones[:], rhs=gain_rows[:], start=True, stop=True)
-        gains = const.tile([P, 2 * HEAD], F32)
-        minus_gains = const.tile([P, 2 * HEAD], F32)
-        nc.vector.tensor_copy(out=gains[:], in_=gain_psum[:])
-        nc.vector.tensor_scalar_mul(out=minus_gains[:], in0=gain_psum[:], scalar1=-1.0)
+        gains = const.tile([P, 2, HALF, 2], F32)
+        nc.vector.tensor_copy(out=gains[:].rearrange("p n i e -> p (n i e)"), in_=gain_psum[:])
+        partner_gains = const.tile([P, 2, HALF, 2], F32)
+        nc.vector.tensor_scalar_mul(out=partner_gains[:, :, :, 0], in0=gains[:, :, :, 1], scalar1=-1.0)
+        nc.vector.tensor_copy(out=partner_gains[:, :, :, 1], in_=gains[:, :, :, 0])
 
         tables = {}
         for n, kind in enumerate(("q", "k")):
+            tables[kind] = []
+            for name, angles, factors in (("same_", cos, gains), ("cross_", sin, partner_gains)):
+                table = const.tile([P, TOKEN_TILES, HALF, 2], F32, name=name + kind)
+                nc.gpsimd.tensor_tensor(
+                    out=table[:],
+                    in0=angles[:].unsqueeze(3).to_broadcast([P, TOKEN_TILES, HALF, 2]),
+                    in1=factors[:, n, :, :].unsqueeze(1).to_broadcast([P, TOKEN_TILES, HALF, 2]),
+                    op=ALU.mult,
+                )
+                tables[kind].append(table)
 
-            def every_second(vector, e):
-                halves = vector[:, HEAD * n : HEAD * (n + 1)].rearrange("p (i e) -> p e i", e=2)
-                return halves[:, e, :].unsqueeze(1).to_broadcast([P, TOKEN_TILES, HALF])
-
-            same = const.tile([P, TOKEN_TILES, 2, HALF], F32, name="same_" + kind)
-            cross = const.tile([P, TOKEN_TILES, 2, HALF], F32, name="cross_" + kind)
-            nc.gpsimd.tensor_tensor(out=same[:, :, 0, :], in0=cos[:], in1=every_second(gains, 0), op=ALU.mult)
-            nc.gpsimd.tensor_tensor(out=same[:, :, 1, :], in0=cos[:], in1=every_second(gains, 1), op=ALU.mult)
-            nc.gpsimd.tensor_tensor(out=cross[:, :, 0, :], in0=sin[:], in1=every_second(minus_gains, 1), op=ALU.mult)
-            nc.gpsimd.tensor_tensor(out=cross[:, :, 1, :], in0=sin[:], in1=every_second(gains, 0), op=ALU.mult)
-            tables[kind] = (same, cross)
-
+        sorted_words = {}
         flipped = {}
         grouped = {}
         codes = {}
         scales = {}
         acc = {}
-        stats = {}
+        sumsq = {}
+        inv_rms = {}
         own = {}
         partner = {}
         result = {}
 
-        def flip(step):
-            kind = operands[step // 2][0]
-            order = ident if kind in ("x", "v") else evens_first
-            words = rows[step // 2][:].bitcast(F32)
-            flipped[step] = []
-            for g in (2 * (step % 2), 2 * (step % 2) + 1):
+        def sort_words(n):
+            sorted_words[n] = stage.tile([P, PASSES, 2, P], F32, name="sorted_words")
+            nc.vector.tensor_copy(
+                out=sorted_words[n][:],
+                in_=rows[n][:, 0, :].bitcast(F32).rearrange("p (g w u) -> p g u w", g=PASSES, u=2),
+            )
+
+        def flip(n):
+            flipped[n] = []
+            for g in range(PASSES):
                 bank = flip_psum.tile([P, 2, 2, P], F32, name="flipped")
                 for b in range(2):
                     for u in range(2):
-                        first = b * (K // 2) + g * (K_PASS // 2)
-                        nc.tensor.transpose(
-                            bank[:, b, u, :], words[:, first + u : first + K_PASS // 2 : 2], order[:]
-                        )
-                flipped[step].append(bank)
+                        if b == 0 and n in sorted_words:
+                            words = sorted_words[n][:, g, u, :]
+                        else:
+                            words = rows[n][:, b, :].bitcast(F32)[:, 2 * P * g + u : 2 * P * (g + 1) : 2]
+                        nc.tensor.transpose(bank[:, b, u, :], words, ident[:])
+                flipped[n].append(bank)
 
-        def regroup(step):
-            grouped[step] = stage.tile([P, 2, 4 * ROWS], BF16, name="grouped", align_bytes=64)
-            for half, bank in enumerate(flipped[step]):
-                out_words = grouped[step][:, half, :].bitcast(F32).rearrange("p (b r u) -> p b r u", b=2, u=2)
-                in_words = bank[:].rearrange("p b u r -> p b r u")
-                if step % 2 == 1 and half == 1:
-                    nc.vector.tensor_copy(out=out_words, in_=in_words)
-                else:
-                    nc.scalar.copy(out=out_words, in_=in_words)
+        def regroup(n, g, engine):
+            if g == 0:
+                grouped[n] = stage.tile([P, PASSES, 4 * ROWS], BF16, name="grouped", align_bytes=64)
+            out_words = grouped[n][:, g, :].bitcast(F32).rearrange("p (b r u) -> p b r u", b=2, u=2)
+            in_words = flipped[n][g][:].rearrange("p b u r -> p b r u")
+            if engine == "scalar":
+                nc.scalar.copy(out=out_words, in_=in_words)
+            else:
+                nc.vector.tensor_copy(out=out_words, in_=in_words)
 
-        def quantise(step):
-            tile_index = step // 2
-            if step % 2 == 0:
-                if operands[tile_index][0] == "x":
-                    codes[tile_index] = const.tile([P, PASSES, ROWS], U32, name="x_codes%d" % tile_index, align_bytes=64)
-                    scales[tile_index] = const.tile([P, PASSES, ROWS], U8, name="x_scales%d" % tile_index, align_bytes=64)
-                else:
-                    codes[tile_index] = w_mx.tile([P, PASSES, ROWS], U32, name="w_codes", align_bytes=64)
-                    scales[tile_index] = w_mx.tile([P, PASSES, ROWS], U8, name="w_scales", align_bytes=64)
-            two_passes = slice(2 * (step % 2), 2 * (step % 2) + 2)
+        def quantise(n, half):
+            if half == 0:
+                pool, name = (const, "x%d" % n) if n in X_TILES else (w_mx, "w")
+                codes[n] = pool.tile([P, PASSES, ROWS], U32, name=name + "_codes", align_bytes=64)
+                scales[n] = pool.tile([P, PASSES, ROWS], U8, name=name + "_scales", align_bytes=64)
+            two_passes = slice(2 * half, 2 * half + 2)
             nc.vector.quantize_mx(
-                out=codes[tile_index][:, two_passes, :].rearrange("p g r -> p (g r)").bitcast(FP8X4),
-                scales=scales[tile_index][:, two_passes, :].rearrange("p g r -> p (g r)"),
-                in_=grouped[step][:].rearrange("p g c -> p (g c)"),
+                out=codes[n][:, two_passes, :].rearrange("p g r -> p (g r)").bitcast(FP8X4),
+                scales=scales[n][:, two_passes, :].rearrange("p g r -> p (g r)"),
+                in_=grouped[n][:, two_passes, :].rearrange("p g c -> p (g c)"),
             )
 
         def multiply(slot):
-            pair, half = slot // 2, slot % 2
-            x_tile = 2 * half
-            w_tile = 1 if pair == 0 else pair + 2
+            xt, wt = X_TILES[slot % 2], w_tile(slot // 2)
             acc[slot] = acc_psum.tile([P, 2, 2 * HEAD], F32, name="acc")
             for jj in range(2):
                 tok = slice(P * jj, P * (jj + 1))
                 for g in range(PASSES):
                     nc.tensor.matmul_mx(
                         out=acc[slot][:, jj, :],
-                        lhsT=codes[x_tile][:, g, tok].bitcast(FP8X4),
-                        lhsT_scale=scales[x_tile][:, g, tok],
-                        rhs=codes[w_tile][:, g, :].bitcast(FP8X4),
-                        rhs_scale=scales[w_tile][:, g, :],
+                        lhsT=codes[xt][:, g, tok].bitcast(FP8X4),
+                        lhsT_scale=scales[xt][:, g, tok],
+                        rhs=codes[wt][:, g, :].bitcast(FP8X4),
+                        rhs_scale=scales[wt][:, g, :],
                         start=(g == 0),
                         stop=(g == PASSES - 1),
                     )
@@ -180,85 +176,56 @@ def tile_slidingcacheattention_pa_kernel(
         def segments(slot):
             half = slot % 2
             return [
-                (acc[slot][:, jj, HEAD * hh : HEAD * (hh + 1)], 4 * half + 2 * jj + hh, TOKEN_TILES * hh + 2 * half + jj)
+                (2 * jj + hh, 2 * half + jj, acc[slot][:, jj, HEAD * hh : HEAD * (hh + 1)])
                 for jj in range(2)
                 for hh in range(2)
             ]
 
         def squares(slot):
-            pair, half = slot // 2, slot % 2
-            if half == 0:
-                stats[pair] = [work.tile([P, 8], F32, name=name) for name in ("sumsq", "rms", "inv_rms")]
-            sumsq, rms, inv_rms = stats[pair]
-            for segment, column, row in segments(slot):
+            sumsq[slot] = work.tile([P, 4], F32, name="sumsq")
+            for s, tile, segment in segments(slot):
                 scratch = work.tile([P, HEAD], F32, name="scratch")
-                nc.scalar.activation(
-                    out=scratch[:], in_=segment, func=ACT.Square, accum_out=sumsq[:, column : column + 1]
-                )
-            these = slice(4 * half, 4 * half + 4)
-            nc.scalar.activation(out=rms[:, these], in_=sumsq[:, these], func=ACT.Sqrt, bias=eps[:], scale=1.0 / HEAD)
+                nc.scalar.activation(out=scratch[:], in_=segment, func=ACT.Square, accum_out=sumsq[slot][:, s : s + 1])
 
-        def invert(slot):
-            sumsq, rms, inv_rms = stats[slot // 2]
-            these = slice(4 * (slot % 2), 4 * (slot % 2) + 4)
-            nc.vector.reciprocal(out=inv_rms[:, these], in_=rms[:, these])
-
-        def slot_rows(tile_of_pair, half):
-            return tile_of_pair[:].rearrange("p (h j) d -> p j h d", h=2)[:, 2 * half : 2 * half + 2, :, :]
+        def norms(slot):
+            inv_rms[slot] = work.tile([P, 4], F32, name="inv_rms")
+            nc.scalar.activation(
+                out=inv_rms[slot][:], in_=sumsq[slot][:], func=ACT.Abs_reciprocal_sqrt, bias=eps[:], scale=1.0 / HEAD
+            )
 
         def products(slot):
-            pair, half = slot // 2, slot % 2
+            own[slot] = work.tile([P, 4, HEAD], F32, name="own")
+            partner[slot] = work.tile([P, 4, HEAD], F32, name="partner")
+            same, cross = tables[pairs[slot // 2][0]]
+            for s, tile, segment in segments(slot):
+                as_pairs = segment.rearrange("p (i e) -> p i e", e=2)
+                for target, factors, table in ((own, as_pairs, same), (partner, as_pairs[:, :, ::-1], cross)):
+                    nc.vector.scalar_tensor_tensor(
+                        out=target[slot][:, s, :].rearrange("p (i e) -> p i e", e=2),
+                        in0=factors,
+                        scalar=inv_rms[slot][:, s : s + 1],
+                        in1=table[:, tile, :, :],
+                        op0=ALU.mult,
+                        op1=ALU.mult,
+                    )
+
+        def slot_rows(pair, half):
             if half == 0:
-                own[pair] = work.tile([P, 2 * TOKEN_TILES, HEAD], F32, name="own")
-                partner[pair] = work.tile([P, 2 * TOKEN_TILES, HEAD], F32, name="partner")
-            same, cross = tables[pairs[pair][0]]
-            tiles = slice(2 * half, 2 * half + 2)
-            sums = acc[slot][:].rearrange("p j (h d) -> p j h d", h=2)
-            nc.vector.tensor_tensor(
-                out=slot_rows(own[pair], half),
-                in0=sums,
-                in1=same[:, tiles, :, :].rearrange("p j e i -> p j (e i)").unsqueeze(2).to_broadcast([P, 2, 2, HEAD]),
-                op=ALU.mult,
-            )
-            for e in range(2):
-                mine = slice(HALF * e, HALF * (e + 1))
-                other = slice(HALF * (1 - e), HALF * (2 - e))
-                nc.vector.tensor_tensor(
-                    out=slot_rows(partner[pair], half)[:, :, :, mine],
-                    in0=sums[:, :, :, other],
-                    in1=cross[:, tiles, e, :].unsqueeze(2).to_broadcast([P, 2, 2, HALF]),
-                    op=ALU.mult,
-                )
+                result[pair] = work.tile([P, 2 * TOKEN_TILES, HEAD], F32, name="result")
+            return result[pair][:].rearrange("p (h j) d -> p j h d", h=2)[:, 2 * half : 2 * half + 2, :, :]
 
         def add(slot):
-            pair, half = slot // 2, slot % 2
             nc.gpsimd.tensor_tensor(
-                out=slot_rows(own[pair], half),
-                in0=slot_rows(own[pair], half),
-                in1=slot_rows(partner[pair], half),
+                out=slot_rows(slot // 2, slot % 2),
+                in0=own[slot][:].rearrange("p (j h) d -> p j h d", h=2),
+                in1=partner[slot][:].rearrange("p (j h) d -> p j h d", h=2),
                 op=ALU.add,
             )
 
-        def finish(slot):
-            pair = slot // 2
-            if slot % 2 == 0:
-                result[pair] = work.tile([P, 2 * TOKEN_TILES, HEAD], F32, name="result")
-            inv_rms = stats[pair][2]
-            for segment, column, row in segments(slot):
-                nc.scalar.activation(
-                    out=result[pair][:, row, :].rearrange("p (i e) -> p i e", e=2),
-                    in_=own[pair][:, row, :].rearrange("p (e i) -> p i e", e=2),
-                    func=ACT.Copy,
-                    scale=inv_rms[:, column : column + 1],
-                )
-
         def copy_v(slot):
-            pair, half = slot // 2, slot % 2
-            if half == 0:
-                result[pair] = work.tile([P, 2 * TOKEN_TILES, HEAD], F32, name="result")
-            out_view = result[pair][:].rearrange("p (h j) d -> p j h d", h=2)[:, 2 * half : 2 * half + 2, :, :]
             in_view = acc[slot][:].rearrange("p j (h d) -> p j h d", h=2)
-            if half == 0:
+            out_view = slot_rows(slot // 2, slot % 2)
+            if slot % 2 == 0:
                 nc.scalar.copy(out=out_view, in_=in_view)
             else:
                 nc.vector.tensor_copy(out=out_view, in_=in_view)
@@ -270,30 +237,50 @@ def tile_slidingcacheattention_pa_kernel(
                 in_=result[pair][:].rearrange("p (h j) d -> p h (j d)", h=2),
             )
 
-        def rotated(slot):
-            return 0 <= slot < SLOTS and pairs[slot // 2][0] != "v"
+        def rotated(pair):
+            return 0 <= pair < PAIRS and pairs[pair][0] != "v"
 
-        for step in range(STEPS):
-            if step < FLIP_STEPS:
-                flip(step)
-            if rotated(step - PRODUCTS_LAG):
-                invert(step - PRODUCTS_LAG)
-                products(step - PRODUCTS_LAG)
-                add(step - PRODUCTS_LAG)
-            if 0 <= step - 1 < FLIP_STEPS:
-                quantise(step - 1)
-            if step < FLIP_STEPS:
-                regroup(step)
-            slot = step - MULTIPLY_LAG
-            if slot >= 0:
-                multiply(slot)
-            if rotated(step - FINISH_LAG):
-                finish(step - FINISH_LAG)
-                if (step - FINISH_LAG) % 2 == 1:
-                    store((step - FINISH_LAG) // 2)
-            if rotated(slot):
-                squares(slot)
-            elif slot >= 0:
-                copy_v(slot)
-                if slot % 2 == 1:
-                    store(slot // 2)
+        for n in range(3):
+            flip(n)
+            for g in range(PASSES):
+                regroup(n, g, "scalar" if g % 2 == 0 else "vector")
+            quantise(n, 0)
+            quantise(n, 1)
+        sort_words(w_tile(1))
+
+        for i in range(PAIRS + 1):
+            n = w_tile(i + 1)
+            more = n < OPERANDS
+            last_a, last_b = 2 * (i - 1), 2 * (i - 1) + 1
+            if more:
+                flip(n)
+            if rotated(i - 1):
+                squares(last_b)
+            if more:
+                regroup(n, 0, "scalar")
+            if rotated(i - 1):
+                norms(last_b)
+                products(last_a)
+                add(last_a)
+            if n + 1 < OPERANDS:
+                sort_words(n + 1)
+            if rotated(i - 1):
+                products(last_b)
+                add(last_b)
+            elif i >= 1:
+                copy_v(last_b)
+            if i >= 1:
+                store(i - 1)
+            if more:
+                for g in range(1, PASSES):
+                    regroup(n, g, "scalar")
+                quantise(n, 0)
+                quantise(n, 1)
+            if i < PAIRS:
+                multiply(2 * i)
+                if rotated(i):
+                    squares(2 * i)
+                    norms(2 * i)
+                else:
+                    copy_v(2 * i)
+                multiply(2 * i + 1)

@@ -50,6 +50,11 @@ def tile_slidingcacheattention_pa_kernel(
         flip_psum = stack.enter_context(tc.psum_pool(name="flip_psum", bufs=4))
         acc_psum = stack.enter_context(tc.psum_pool(name="acc_psum", bufs=4))
 
+        x_view = x[0].rearrange("(p j) k -> p j k", j=TOKEN_TILES)
+        rows = [rows_pool.tile([P, 2, K], BF16, name="loaded")]
+        for half in (slice(0, K // 2), slice(K // 2, K)):
+            nc.sync.dma_start(out=rows[0][:, :, half], in_=x_view[:, 0:2, half])
+
         cos = const.tile([P, TOKEN_TILES, HALF], BF16)
         sin = const.tile([P, TOKEN_TILES, HALF], BF16)
         gain_rows = const.tile([P, 2 * HEAD], BF16)
@@ -59,14 +64,12 @@ def tile_slidingcacheattention_pa_kernel(
         nc.sync.dma_start(out=cos[:], in_=freqs_cos.rearrange("(p j) i -> p j i", j=TOKEN_TILES))
         nc.sync.dma_start(out=sin[:], in_=freqs_sin.rearrange("(p j) i -> p j i", j=TOKEN_TILES))
 
-        x_view = x[0].rearrange("(p j) k -> p j k", j=TOKEN_TILES)
         pairs = [("q", Wq, out_0, n) for n in range(Q_PAIRS)]
         pairs.extend([("k", Wk, out_1, n) for n in range(K_PAIRS)])
         pairs.extend([("v", Wv, out_2, n) for n in range(V_PAIRS)])
         pair_views = [w[ROWS * n : ROWS * (n + 1), :].rearrange("(b p) k -> p b k", p=P) for (kind, w, out, n) in pairs]
-        views = [x_view[:, 0:2, :], pair_views[0], x_view[:, 2:4, :]]
+        views = [pair_views[0], x_view[:, 2:4, :]]
         views.extend(pair_views[1:])
-        rows = []
         for view in views:
             loaded = rows_pool.tile([P, 2, K], BF16, name="loaded")
             nc.sync.dma_start(out=loaded[:], in_=view)
@@ -82,26 +85,28 @@ def tile_slidingcacheattention_pa_kernel(
 
         ones = const.tile([P, P], BF16)
         nc.vector.memset(ones[:], 1.0)
-        gain_psum = flip_psum.tile([P, 2 * HEAD], F32, tag="flipped")
-        nc.tensor.matmul(out=gain_psum[:], lhsT=ones[:], rhs=gain_rows[:], start=True, stop=True)
         gains = const.tile([P, 2, HALF, 2], F32)
-        nc.vector.tensor_copy(out=gains[:].rearrange("p n i e -> p (n i e)"), in_=gain_psum[:])
         partner_gains = const.tile([P, 2, HALF, 2], F32)
-        nc.vector.tensor_scalar_mul(out=partner_gains[:, :, :, 0], in0=gains[:, :, :, 1], scalar1=-1.0)
-        nc.vector.tensor_copy(out=partner_gains[:, :, :, 1], in_=gains[:, :, :, 0])
 
         tables = {}
-        for n, kind in enumerate(("q", "k")):
-            tables[kind] = []
-            for name, angles, factors in (("same_", cos, gains), ("cross_", sin, partner_gains)):
-                table = const.tile([P, TOKEN_TILES, HALF, 2], F32, name=name + kind)
-                nc.gpsimd.tensor_tensor(
-                    out=table[:],
-                    in0=angles[:].unsqueeze(3).to_broadcast([P, TOKEN_TILES, HALF, 2]),
-                    in1=factors[:, n, :, :].unsqueeze(1).to_broadcast([P, TOKEN_TILES, HALF, 2]),
-                    op=ALU.mult,
-                )
-                tables[kind].append(table)
+
+        def make_tables():
+            gain_psum = acc_psum.tile([P, 2 * HEAD], F32, tag="acc")
+            nc.tensor.matmul(out=gain_psum[:], lhsT=ones[:], rhs=gain_rows[:], start=True, stop=True)
+            nc.vector.tensor_copy(out=gains[:].rearrange("p n i e -> p (n i e)"), in_=gain_psum[:])
+            nc.vector.tensor_scalar_mul(out=partner_gains[:, :, :, 0], in0=gains[:, :, :, 1], scalar1=-1.0)
+            nc.vector.tensor_copy(out=partner_gains[:, :, :, 1], in_=gains[:, :, :, 0])
+            for n, kind in enumerate(("q", "k")):
+                tables[kind] = []
+                for name, angles, factors in (("same_", cos, gains), ("cross_", sin, partner_gains)):
+                    table = const.tile([P, TOKEN_TILES, HALF, 2], F32, name=name + kind)
+                    nc.gpsimd.tensor_tensor(
+                        out=table[:],
+                        in0=angles[:].unsqueeze(3).to_broadcast([P, TOKEN_TILES, HALF, 2]),
+                        in1=factors[:, n, :, :].unsqueeze(1).to_broadcast([P, TOKEN_TILES, HALF, 2]),
+                        op=ALU.mult,
+                    )
+                    tables[kind].append(table)
 
         sorted_words = {}
         flipped = {}
@@ -243,15 +248,22 @@ def tile_slidingcacheattention_pa_kernel(
         for n in range(3):
             flip(n)
             for g in range(PASSES):
-                regroup(n, g, "scalar" if g % 2 == 0 else "vector")
+                regroup(n, g, "vector" if g == 1 else "scalar")
+            if n == 2:
+                sort_words(w_tile(1))
             quantise(n, 0)
             quantise(n, 1)
-        sort_words(w_tile(1))
+            if n == 0:
+                make_tables()
 
         for i in range(PAIRS + 1):
             n = w_tile(i + 1)
             more = n < OPERANDS
             last_a, last_b = 2 * (i - 1), 2 * (i - 1) + 1
+            if i == 0:
+                multiply(0)
+                squares(0)
+                norms(0)
             if more:
                 flip(n)
             if rotated(i - 1):
@@ -277,10 +289,11 @@ def tile_slidingcacheattention_pa_kernel(
                 quantise(n, 0)
                 quantise(n, 1)
             if i < PAIRS:
-                multiply(2 * i)
-                if rotated(i):
-                    squares(2 * i)
-                    norms(2 * i)
-                else:
-                    copy_v(2 * i)
+                if i > 0:
+                    multiply(2 * i)
+                    if rotated(i):
+                        squares(2 * i)
+                        norms(2 * i)
+                    else:
+                        copy_v(2 * i)
                 multiply(2 * i + 1)

@@ -45,6 +45,7 @@ def tile_slidingcacheattention_pa_kernel(
         const = stack.enter_context(tc.tile_pool(name="const", bufs=1))
         rows_pool = stack.enter_context(tc.tile_pool(name="rows", bufs=OPERANDS))
         stage = stack.enter_context(tc.tile_pool(name="stage", bufs=2))
+        sorted_pool = stack.enter_context(tc.tile_pool(name="sorted_pool", bufs=3))
         w_mx = stack.enter_context(tc.tile_pool(name="w_mx", bufs=3))
         work = stack.enter_context(tc.tile_pool(name="work", bufs=4))
         flip_psum = stack.enter_context(tc.psum_pool(name="flip_psum", bufs=4))
@@ -86,7 +87,7 @@ def tile_slidingcacheattention_pa_kernel(
         ones = const.tile([P, P], BF16)
         nc.vector.memset(ones[:], 1.0)
         gains = const.tile([P, 2, HALF, 2], F32)
-        partner_gains = const.tile([P, 2, HALF, 2], F32)
+        signed_gains = const.tile([P, 2, HALF, 2], F32)
 
         tables = {}
 
@@ -94,19 +95,17 @@ def tile_slidingcacheattention_pa_kernel(
             gain_psum = acc_psum.tile([P, 2 * HEAD], F32, tag="acc")
             nc.tensor.matmul(out=gain_psum[:], lhsT=ones[:], rhs=gain_rows[:], start=True, stop=True)
             nc.vector.tensor_copy(out=gains[:].rearrange("p n i e -> p (n i e)"), in_=gain_psum[:])
-            nc.vector.tensor_scalar_mul(out=partner_gains[:, :, :, 0], in0=gains[:, :, :, 1], scalar1=-1.0)
-            nc.vector.tensor_copy(out=partner_gains[:, :, :, 1], in_=gains[:, :, :, 0])
+            nc.vector.tensor_copy(out=signed_gains[:, :, :, 0], in_=gains[:, :, :, 0])
+            nc.vector.tensor_scalar_mul(out=signed_gains[:, :, :, 1], in0=gains[:, :, :, 1], scalar1=-1.0)
             for n, kind in enumerate(("q", "k")):
-                tables[kind] = []
-                for name, angles, factors in (("same_", cos, gains), ("cross_", sin, partner_gains)):
-                    table = const.tile([P, TOKEN_TILES, HALF, 2], F32, name=name + kind)
+                tables[kind] = const.tile([P, TOKEN_TILES, 2, HALF, 2], F32, name="table_" + kind)
+                for place, angles, factors in ((0, cos, gains), (1, sin, signed_gains)):
                     nc.gpsimd.tensor_tensor(
-                        out=table[:],
+                        out=tables[kind][:, :, place, :, :],
                         in0=angles[:].unsqueeze(3).to_broadcast([P, TOKEN_TILES, HALF, 2]),
                         in1=factors[:, n, :, :].unsqueeze(1).to_broadcast([P, TOKEN_TILES, HALF, 2]),
                         op=ALU.mult,
                     )
-                    tables[kind].append(table)
 
         sorted_words = {}
         flipped = {}
@@ -116,12 +115,11 @@ def tile_slidingcacheattention_pa_kernel(
         acc = {}
         sumsq = {}
         inv_rms = {}
-        own = {}
-        partner = {}
+        terms = {}
         result = {}
 
         def sort_words(n):
-            sorted_words[n] = stage.tile([P, PASSES, 2, P], F32, name="sorted_words")
+            sorted_words[n] = sorted_pool.tile([P, PASSES, 2, P], F32, name="sorted_words")
             nc.vector.tensor_copy(
                 out=sorted_words[n][:],
                 in_=rows[n][:, 0, :].bitcast(F32).rearrange("p (g w u) -> p g u w", g=PASSES, u=2),
@@ -199,20 +197,17 @@ def tile_slidingcacheattention_pa_kernel(
             )
 
         def products(slot):
-            own[slot] = work.tile([P, 4, HEAD], F32, name="own")
-            partner[slot] = work.tile([P, 4, HEAD], F32, name="partner")
-            same, cross = tables[pairs[slot // 2][0]]
+            terms[slot] = work.tile([P, 4, 2, HEAD], F32, name="terms")
+            table = tables[pairs[slot // 2][0]]
             for s, tile, segment in segments(slot):
-                as_pairs = segment.rearrange("p (i e) -> p i e", e=2)
-                for target, factors, table in ((own, as_pairs, same), (partner, as_pairs[:, :, ::-1], cross)):
-                    nc.vector.scalar_tensor_tensor(
-                        out=target[slot][:, s, :].rearrange("p (i e) -> p i e", e=2),
-                        in0=factors,
-                        scalar=inv_rms[slot][:, s : s + 1],
-                        in1=table[:, tile, :, :],
-                        op0=ALU.mult,
-                        op1=ALU.mult,
-                    )
+                nc.vector.scalar_tensor_tensor(
+                    out=terms[slot][:, s, :, :],
+                    in0=segment.unsqueeze(1).to_broadcast([P, 2, HEAD]),
+                    scalar=inv_rms[slot][:, s : s + 1],
+                    in1=table[:, tile, :, :, :].rearrange("p v i e -> p v (i e)"),
+                    op0=ALU.mult,
+                    op1=ALU.mult,
+                )
 
         def slot_rows(pair, half):
             if half == 0:
@@ -221,9 +216,9 @@ def tile_slidingcacheattention_pa_kernel(
 
         def add(slot):
             nc.gpsimd.tensor_tensor(
-                out=slot_rows(slot // 2, slot % 2),
-                in0=own[slot][:].rearrange("p (j h) d -> p j h d", h=2),
-                in1=partner[slot][:].rearrange("p (j h) d -> p j h d", h=2),
+                out=slot_rows(slot // 2, slot % 2).rearrange("p j h (i e) -> p j h i e", e=2),
+                in0=terms[slot][:, :, 0, :].rearrange("p (j h) (i e) -> p j h i e", h=2, e=2),
+                in1=terms[slot][:, :, 1, :].rearrange("p (j h) (i e) -> p j h i e", h=2, e=2)[:, :, :, :, ::-1],
                 op=ALU.add,
             )
 
@@ -255,6 +250,7 @@ def tile_slidingcacheattention_pa_kernel(
             quantise(n, 1)
             if n == 0:
                 make_tables()
+        sort_words(w_tile(2))
 
         for i in range(PAIRS + 1):
             n = w_tile(i + 1)
@@ -264,6 +260,9 @@ def tile_slidingcacheattention_pa_kernel(
                 multiply(0)
                 squares(0)
                 norms(0)
+            elif i < PAIRS:
+                quantise(w_tile(i), 0)
+                quantise(w_tile(i), 1)
             if more:
                 flip(n)
             if rotated(i - 1):
@@ -274,9 +273,6 @@ def tile_slidingcacheattention_pa_kernel(
                 norms(last_b)
                 products(last_a)
                 add(last_a)
-            if n + 1 < OPERANDS:
-                sort_words(n + 1)
-            if rotated(i - 1):
                 products(last_b)
                 add(last_b)
             elif i >= 1:
@@ -286,8 +282,8 @@ def tile_slidingcacheattention_pa_kernel(
             if more:
                 for g in range(1, PASSES):
                     regroup(n, g, "scalar")
-                quantise(n, 0)
-                quantise(n, 1)
+            if n + 2 < OPERANDS:
+                sort_words(n + 2)
             if i < PAIRS:
                 if i > 0:
                     multiply(2 * i)

@@ -48,13 +48,14 @@ def tile_slidingcacheattention_pa_kernel(
         sorted_pool = stack.enter_context(tc.tile_pool(name="sorted_pool", bufs=3))
         w_mx = stack.enter_context(tc.tile_pool(name="w_mx", bufs=3))
         work = stack.enter_context(tc.tile_pool(name="work", bufs=4))
+        terms_pool = stack.enter_context(tc.tile_pool(name="terms_pool", bufs=2))
         flip_psum = stack.enter_context(tc.psum_pool(name="flip_psum", bufs=4))
         acc_psum = stack.enter_context(tc.psum_pool(name="acc_psum", bufs=4))
 
         x_view = x[0].rearrange("(p j) k -> p j k", j=TOKEN_TILES)
         rows = [rows_pool.tile([P, 2, K], BF16, name="loaded")]
-        for half in (slice(0, K // 2), slice(K // 2, K)):
-            nc.sync.dma_start(out=rows[0][:, :, half], in_=x_view[:, 0:2, half])
+        for b in range(2):
+            nc.sync.dma_start(out=rows[0][:, b, :], in_=x_view[:, b, :])
 
         cos = const.tile([P, TOKEN_TILES, HALF], BF16)
         sin = const.tile([P, TOKEN_TILES, HALF], BF16)
@@ -73,7 +74,11 @@ def tile_slidingcacheattention_pa_kernel(
         views.extend(pair_views[1:])
         for view in views:
             loaded = rows_pool.tile([P, 2, K], BF16, name="loaded")
-            nc.sync.dma_start(out=loaded[:], in_=view)
+            if len(rows) < 3:
+                for b in range(2):
+                    nc.sync.dma_start(out=loaded[:, b, :], in_=view[:, b, :])
+            else:
+                nc.sync.dma_start(out=loaded[:], in_=view)
             rows.append(loaded)
 
         eps = const.tile([P, 1], F32)
@@ -125,24 +130,29 @@ def tile_slidingcacheattention_pa_kernel(
                 in_=rows[n][:, 0, :].bitcast(F32).rearrange("p (g w u) -> p g u w", g=PASSES, u=2),
             )
 
+        banks = [(0, 0), (0, 2), (1, 0), (1, 2)]
+
         def flip(n):
             flipped[n] = []
-            for g in range(PASSES):
+            for b, first in banks:
                 bank = flip_psum.tile([P, 2, 2, P], F32, name="flipped")
-                for b in range(2):
+                for g in range(2):
                     for u in range(2):
                         if b == 0 and n in sorted_words:
-                            words = sorted_words[n][:, g, u, :]
+                            words = sorted_words[n][:, first + g, u, :]
                         else:
-                            words = rows[n][:, b, :].bitcast(F32)[:, 2 * P * g + u : 2 * P * (g + 1) : 2]
-                        nc.tensor.transpose(bank[:, b, u, :], words, ident[:])
+                            word = 2 * P * (first + g)
+                            words = rows[n][:, b, :].bitcast(F32)[:, word + u : word + 2 * P : 2]
+                        nc.tensor.transpose(bank[:, g, u, :], words, ident[:])
                 flipped[n].append(bank)
 
-        def regroup(n, g, engine):
-            if g == 0:
-                grouped[n] = stage.tile([P, PASSES, 4 * ROWS], BF16, name="grouped", align_bytes=64)
-            out_words = grouped[n][:, g, :].bitcast(F32).rearrange("p (b r u) -> p b r u", b=2, u=2)
-            in_words = flipped[n][g][:].rearrange("p b u r -> p b r u")
+        def regroup(n, k, engine):
+            if k == 0:
+                grouped[n] = stage.tile([P, PASSES, ROWS, 4], BF16, name="grouped", align_bytes=64)
+            b, first = banks[k]
+            out_rows = grouped[n][:, first : first + 2, P * b : P * (b + 1), :]
+            out_words = out_rows.rearrange("p g r t -> p g (r t)").bitcast(F32).rearrange("p g (r u) -> p g r u", u=2)
+            in_words = flipped[n][k][:].rearrange("p g u r -> p g r u")
             if engine == "scalar":
                 nc.scalar.copy(out=out_words, in_=in_words)
             else:
@@ -157,7 +167,7 @@ def tile_slidingcacheattention_pa_kernel(
             nc.vector.quantize_mx(
                 out=codes[n][:, two_passes, :].rearrange("p g r -> p (g r)").bitcast(FP8X4),
                 scales=scales[n][:, two_passes, :].rearrange("p g r -> p (g r)"),
-                in_=grouped[n][:, two_passes, :].rearrange("p g c -> p (g c)"),
+                in_=grouped[n][:, two_passes, :, :].rearrange("p g r t -> p (g r t)"),
             )
 
         def multiply(slot):
@@ -197,11 +207,13 @@ def tile_slidingcacheattention_pa_kernel(
             )
 
         def products(slot):
-            terms[slot] = work.tile([P, 4, 2, HEAD], F32, name="terms")
-            table = tables[pairs[slot // 2][0]]
+            pair = slot // 2
+            if slot % 2 == 0:
+                terms[pair] = terms_pool.tile([P, 2 * TOKEN_TILES, 2, HEAD], F32, name="terms")
+            table = tables[pairs[pair][0]]
             for s, tile, segment in segments(slot):
                 nc.vector.scalar_tensor_tensor(
-                    out=terms[slot][:, s, :, :],
+                    out=terms[pair][:, TOKEN_TILES * (s % 2) + tile, :, :],
                     in0=segment.unsqueeze(1).to_broadcast([P, 2, HEAD]),
                     scalar=inv_rms[slot][:, s : s + 1],
                     in1=table[:, tile, :, :, :].rearrange("p v i e -> p v (i e)"),
@@ -209,32 +221,29 @@ def tile_slidingcacheattention_pa_kernel(
                     op1=ALU.mult,
                 )
 
-        def slot_rows(pair, half):
-            if half == 0:
-                result[pair] = work.tile([P, 2 * TOKEN_TILES, HEAD], F32, name="result")
-            return result[pair][:].rearrange("p (h j) d -> p j h d", h=2)[:, 2 * half : 2 * half + 2, :, :]
-
-        def add(slot):
-            nc.gpsimd.tensor_tensor(
-                out=slot_rows(slot // 2, slot % 2).rearrange("p j h (i e) -> p j h i e", e=2),
-                in0=terms[slot][:, :, 0, :].rearrange("p (j h) (i e) -> p j h i e", h=2, e=2),
-                in1=terms[slot][:, :, 1, :].rearrange("p (j h) (i e) -> p j h i e", h=2, e=2)[:, :, :, :, ::-1],
-                op=ALU.add,
+        def add(pair, engine):
+            result[pair] = work.tile([P, 2 * TOKEN_TILES, HEAD], F32, name="result")
+            own, other = [terms[pair][:, :, v, :].rearrange("p r (i e) -> p r i e", e=2) for v in range(2)]
+            engine.tensor_tensor(
+                out=result[pair][:].rearrange("p r (i e) -> p r i e", e=2), in0=own, in1=other[:, :, :, ::-1], op=ALU.add
             )
 
         def copy_v(slot):
+            pair, half = slot // 2, slot % 2
+            if half == 0:
+                result[pair] = work.tile([P, 2 * TOKEN_TILES, HEAD], F32, name="result")
             in_view = acc[slot][:].rearrange("p j (h d) -> p j h d", h=2)
-            out_view = slot_rows(slot // 2, slot % 2)
-            if slot % 2 == 0:
+            out_view = result[pair][:].rearrange("p (h j) d -> p j h d", h=2)[:, 2 * half : 2 * half + 2, :, :]
+            if half == 0:
                 nc.scalar.copy(out=out_view, in_=in_view)
             else:
                 nc.vector.tensor_copy(out=out_view, in_=in_view)
 
-        def store(pair):
+        def store(pair, tiles):
             kind, w, out, n = pairs[pair]
             nc.sync.dma_start(
-                out=out[0, 2 * n : 2 * n + 2].rearrange("h (p j) d -> p h (j d)", j=TOKEN_TILES),
-                in_=result[pair][:].rearrange("p (h j) d -> p h (j d)", h=2),
+                out=out[0, 2 * n : 2 * n + 2].rearrange("h (p j) d -> p h j d", j=TOKEN_TILES)[:, :, tiles, :],
+                in_=result[pair][:].rearrange("p (h j) d -> p h j d", h=2)[:, :, tiles, :],
             )
 
         def rotated(pair):
@@ -242,10 +251,8 @@ def tile_slidingcacheattention_pa_kernel(
 
         for n in range(3):
             flip(n)
-            for g in range(PASSES):
-                regroup(n, g, "vector" if g == 1 else "scalar")
-            if n == 2:
-                sort_words(w_tile(1))
+            for k in range(len(banks)):
+                regroup(n, k, "vector" if k == 1 else "scalar")
             quantise(n, 0)
             quantise(n, 1)
             if n == 0:
@@ -263,6 +270,9 @@ def tile_slidingcacheattention_pa_kernel(
             elif i < PAIRS:
                 quantise(w_tile(i), 0)
                 quantise(w_tile(i), 1)
+            if rotated(i - 2) and not rotated(i - 1):
+                add(i - 2, nc.vector)
+                store(i - 2, slice(0, TOKEN_TILES))
             if more:
                 flip(n)
             if rotated(i - 1):
@@ -272,16 +282,16 @@ def tile_slidingcacheattention_pa_kernel(
             if rotated(i - 1):
                 norms(last_b)
                 products(last_a)
-                add(last_a)
                 products(last_b)
-                add(last_b)
+                if rotated(i):
+                    add(i - 1, nc.gpsimd)
+                    store(i - 1, slice(0, TOKEN_TILES))
             elif i >= 1:
                 copy_v(last_b)
-            if i >= 1:
-                store(i - 1)
+                store(i - 1, slice(2, 4))
             if more:
-                for g in range(1, PASSES):
-                    regroup(n, g, "scalar")
+                for k in range(1, len(banks)):
+                    regroup(n, k, "scalar")
             if n + 2 < OPERANDS:
                 sort_words(n + 2)
             if i < PAIRS:
@@ -292,4 +302,5 @@ def tile_slidingcacheattention_pa_kernel(
                         norms(2 * i)
                     else:
                         copy_v(2 * i)
+                        store(i, slice(0, 2))
                 multiply(2 * i + 1)

@@ -18,6 +18,8 @@ K = 2048
 K_PASS = 4 * P
 PASSES = K // K_PASS
 WORDS = K // 2
+BLOCK = 32
+FIRST_TURNED = 4
 HEAD = 128
 HALF = HEAD // 2
 ROWS = 2 * P
@@ -33,6 +35,8 @@ def w_tile(pair):
     return 1 if pair == 0 else pair + 2
 
 
+SLOTS = 2 * PAIRS
+
 FLOPS = 2 * TOKENS * K * HEAD * 2 * PAIRS
 
 
@@ -45,9 +49,9 @@ def tile_slidingcacheattention_pa_kernel(
         const = stack.enter_context(tc.tile_pool(name="const", bufs=1))
         rows_pool = stack.enter_context(tc.tile_pool(name="rows", bufs=OPERANDS))
         stage = stack.enter_context(tc.tile_pool(name="stage", bufs=2))
-        sorted_pool = stack.enter_context(tc.tile_pool(name="sorted_pool", bufs=3))
         w_mx = stack.enter_context(tc.tile_pool(name="w_mx", bufs=3))
         work = stack.enter_context(tc.tile_pool(name="work", bufs=4))
+        turn_pool = stack.enter_context(tc.tile_pool(name="turn_pool", bufs=3))
         terms_pool = stack.enter_context(tc.tile_pool(name="terms_pool", bufs=2))
         flip_psum = stack.enter_context(tc.psum_pool(name="flip_psum", bufs=4))
         acc_psum = stack.enter_context(tc.psum_pool(name="acc_psum", bufs=4))
@@ -74,11 +78,17 @@ def tile_slidingcacheattention_pa_kernel(
         views.extend(pair_views[1:])
         for view in views:
             loaded = rows_pool.tile([P, 2, K], BF16, name="loaded")
-            if len(rows) < 3:
-                for b in range(2):
-                    nc.sync.dma_start(out=loaded[:, b, :], in_=view[:, b, :])
-            else:
-                nc.sync.dma_start(out=loaded[:], in_=view)
+            n = len(rows)
+            end = K - K_PASS if n >= FIRST_TURNED else K
+            nc.sync.dma_start(out=loaded[:, 0, :], in_=view[:, 0, :])
+            nc.sync.dma_start(out=loaded[:, 1, :end], in_=view[:, 1, :end])
+            if end < K:
+                kind, w, out, m = pairs[n - 2 if n > 2 else 0]
+                quarters = w[ROWS * m + P : ROWS * (m + 1), end:K].rearrange("(r i) (q k) -> q i r k", i=BLOCK, q=4)
+                for q in range(4):
+                    nc.sync.dma_start(
+                        out=loaded[BLOCK * q : BLOCK * (q + 1), 1, end:K].rearrange("p (r k) -> p r k", r=4), in_=quarters[q]
+                    )
             rows.append(loaded)
 
         eps = const.tile([P, 1], F32)
@@ -112,7 +122,8 @@ def tile_slidingcacheattention_pa_kernel(
                         op=ALU.mult,
                     )
 
-        sorted_words = {}
+        ordered = {}
+        turned = {}
         flipped = {}
         grouped = {}
         codes = {}
@@ -123,13 +134,6 @@ def tile_slidingcacheattention_pa_kernel(
         terms = {}
         result = {}
 
-        def sort_words(n):
-            sorted_words[n] = sorted_pool.tile([P, PASSES, 2, P], F32, name="sorted_words")
-            nc.vector.tensor_copy(
-                out=sorted_words[n][:],
-                in_=rows[n][:, 0, :].bitcast(F32).rearrange("p (g w u) -> p g u w", g=PASSES, u=2),
-            )
-
         banks = [(0, 0), (0, 2), (1, 0), (1, 2)]
 
         def flip(n):
@@ -137,19 +141,39 @@ def tile_slidingcacheattention_pa_kernel(
             for b, first in banks:
                 bank = flip_psum.tile([P, 2, 2, P], F32, name="flipped")
                 for g in range(2):
+                    if n >= FIRST_TURNED and b == 1 and first + g == PASSES - 1:
+                        continue
                     for u in range(2):
-                        if b == 0 and n in sorted_words:
-                            words = sorted_words[n][:, first + g, u, :]
-                        else:
-                            word = 2 * P * (first + g)
-                            words = rows[n][:, b, :].bitcast(F32)[:, word + u : word + 2 * P : 2]
+                        word = 2 * P * (first + g)
+                        words = rows[n][:, b, :].bitcast(F32)[:, word + u : word + 2 * P : 2]
                         nc.tensor.transpose(bank[:, g, u, :], words, ident[:])
                 flipped[n].append(bank)
+
+        def order_words(n):
+            ordered[n] = turn_pool.tile([P, 4, 2, BLOCK], F32, name="ordered", align_bytes=64)
+            raw = rows[n][:, 1, K - K_PASS : K].bitcast(F32)
+            nc.vector.tensor_copy(out=ordered[n][:], in_=raw.rearrange("p (r j u) -> p r u j", r=4, u=2))
+
+        def turn(n):
+            turned[n] = turn_pool.tile([P, 4, 2, BLOCK], F32, name="turned", align_bytes=64)
+            nc.vector.transpose(
+                out=turned[n][:].rearrange("p r u i -> p (r u i)"), in_=ordered[n][:].rearrange("p r u j -> p (r u j)")
+            )
 
         def regroup(n, k, engine):
             if k == 0:
                 grouped[n] = stage.tile([P, PASSES, ROWS, 4], BF16, name="grouped", align_bytes=64)
             b, first = banks[k]
+            if n >= FIRST_TURNED and k == 3:
+                out_words = grouped[n][:, first, P:, :].rearrange("p r t -> p (r t)").bitcast(F32)
+                nc.scalar.copy(
+                    out=out_words.rearrange("p (r u) -> p r u", u=2), in_=flipped[n][k][:, 0, :, :].rearrange("p u r -> p r u")
+                )
+                out_words = grouped[n][:, first + 1, P:, :].rearrange("p r t -> p (r t)").bitcast(F32)
+                nc.scalar.copy(
+                    out=out_words.rearrange("p (r i u) -> p r i u", r=4, u=2), in_=turned[n][:].rearrange("p r u i -> p r i u")
+                )
+                return
             out_rows = grouped[n][:, first : first + 2, P * b : P * (b + 1), :]
             out_words = out_rows.rearrange("p g r t -> p g (r t)").bitcast(F32).rearrange("p g (r u) -> p g r u", u=2)
             in_words = flipped[n][k][:].rearrange("p g u r -> p g r u")
@@ -172,12 +196,19 @@ def tile_slidingcacheattention_pa_kernel(
 
         def multiply(slot):
             xt, wt = X_TILES[slot % 2], w_tile(slot // 2)
-            acc[slot] = acc_psum.tile([P, 2, 2 * HEAD], F32, name="acc")
+            if slot < SLOTS - 1:
+                bank = acc_psum.tile([P, 2, 2 * HEAD], F32, name="acc")
+                acc[slot] = [bank[:, jj, :] for jj in range(2)]
+            else:
+                acc[slot] = []
+                for jj in range(2):
+                    bank = flip_psum.tile([P, 2 * HEAD], F32, tag="flipped")
+                    acc[slot].append(bank[:])
             for jj in range(2):
                 tok = slice(P * jj, P * (jj + 1))
                 for g in range(PASSES):
                     nc.tensor.matmul_mx(
-                        out=acc[slot][:, jj, :],
+                        out=acc[slot][jj],
                         lhsT=codes[xt][:, g, tok].bitcast(FP8X4),
                         lhsT_scale=scales[xt][:, g, tok],
                         rhs=codes[wt][:, g, :].bitcast(FP8X4),
@@ -189,7 +220,7 @@ def tile_slidingcacheattention_pa_kernel(
         def segments(slot):
             half = slot % 2
             return [
-                (2 * jj + hh, 2 * half + jj, acc[slot][:, jj, HEAD * hh : HEAD * (hh + 1)])
+                (2 * jj + hh, 2 * half + jj, acc[slot][jj][:, HEAD * hh : HEAD * (hh + 1)])
                 for jj in range(2)
                 for hh in range(2)
             ]
@@ -221,29 +252,43 @@ def tile_slidingcacheattention_pa_kernel(
                     op1=ALU.mult,
                 )
 
-        def add(pair, engine):
+        def begin_result(pair):
             result[pair] = work.tile([P, 2 * TOKEN_TILES, HEAD], F32, name="result")
-            own, other = [terms[pair][:, :, v, :].rearrange("p r (i e) -> p r i e", e=2) for v in range(2)]
+            nc.vector.memset(result[pair][:, 0, 0:1], 0.0)
+
+        def add(pair, engine, some):
+            own, other = [terms[pair][:, some, v, :].rearrange("p r (i e) -> p r i e", e=2) for v in range(2)]
             engine.tensor_tensor(
-                out=result[pair][:].rearrange("p r (i e) -> p r i e", e=2), in0=own, in1=other[:, :, :, ::-1], op=ALU.add
+                out=result[pair][:, some, :].rearrange("p r (i e) -> p r i e", e=2),
+                in0=own,
+                in1=other[:, :, :, ::-1],
+                op=ALU.add,
             )
 
         def copy_v(slot):
             pair, half = slot // 2, slot % 2
             if half == 0:
                 result[pair] = work.tile([P, 2 * TOKEN_TILES, HEAD], F32, name="result")
-            in_view = acc[slot][:].rearrange("p j (h d) -> p j h d", h=2)
-            out_view = result[pair][:].rearrange("p (h j) d -> p j h d", h=2)[:, 2 * half : 2 * half + 2, :, :]
-            if half == 0:
-                nc.scalar.copy(out=out_view, in_=in_view)
-            else:
-                nc.vector.tensor_copy(out=out_view, in_=in_view)
+            for jj in range(2):
+                out_view = result[pair][:].rearrange("p (h j) d -> p j h d", h=2)[:, 2 * half + jj, :, :]
+                in_view = acc[slot][jj].rearrange("p (h d) -> p h d", h=2)
+                if half == 0 or (slot == SLOTS - 1 and jj == 0):
+                    nc.scalar.copy(out=out_view, in_=in_view)
+                else:
+                    nc.vector.tensor_copy(out=out_view, in_=in_view)
 
         def store(pair, tiles):
             kind, w, out, n = pairs[pair]
             nc.sync.dma_start(
                 out=out[0, 2 * n : 2 * n + 2].rearrange("h (p j) d -> p h j d", j=TOKEN_TILES)[:, :, tiles, :],
                 in_=result[pair][:].rearrange("p (h j) d -> p h j d", h=2)[:, :, tiles, :],
+            )
+
+        def store_head(pair, h):
+            kind, w, out, n = pairs[pair]
+            nc.sync.dma_start(
+                out=out[0, 2 * n + h].rearrange("(p j) d -> p j d", j=TOKEN_TILES),
+                in_=result[pair][:, TOKEN_TILES * h : TOKEN_TILES * (h + 1), :],
             )
 
         def rotated(pair):
@@ -257,22 +302,33 @@ def tile_slidingcacheattention_pa_kernel(
             quantise(n, 1)
             if n == 0:
                 make_tables()
-        sort_words(w_tile(2))
 
         for i in range(PAIRS + 1):
-            n = w_tile(i + 1)
+            n = w_tile(i + 1) if i > 0 else 3
             more = n < OPERANDS
             last_a, last_b = 2 * (i - 1), 2 * (i - 1) + 1
             if i == 0:
                 multiply(0)
                 squares(0)
                 norms(0)
-            elif i < PAIRS:
+            last_rotated = rotated(i - 2) and not rotated(i - 1)
+            if last_rotated:
+                result[i - 2] = work.tile([P, 2 * TOKEN_TILES, HEAD], F32, name="result")
+                add(i - 2, nc.vector, slice(0, TOKEN_TILES))
+                store_head(i - 2, 0)
+            if 1 <= i < PAIRS:
                 quantise(w_tile(i), 0)
                 quantise(w_tile(i), 1)
-            if rotated(i - 2) and not rotated(i - 1):
-                add(i - 2, nc.vector)
-                store(i - 2, slice(0, TOKEN_TILES))
+            if last_rotated:
+                add(i - 2, nc.vector, slice(TOKEN_TILES, 2 * TOKEN_TILES))
+                store_head(i - 2, 1)
+            if n + 1 < OPERANDS:
+                order_words(n + 1)
+            if rotated(i - 2) and not last_rotated:
+                begin_result(i - 2)
+                add(i - 2, nc.gpsimd, slice(0, 2 * TOKEN_TILES))
+                store_head(i - 2, 0)
+                store_head(i - 2, 1)
             if more:
                 flip(n)
             if rotated(i - 1):
@@ -282,18 +338,21 @@ def tile_slidingcacheattention_pa_kernel(
             if rotated(i - 1):
                 norms(last_b)
                 products(last_a)
+                if n + 1 < OPERANDS:
+                    turn(n + 1)
                 products(last_b)
-                if rotated(i):
-                    add(i - 1, nc.gpsimd)
-                    store(i - 1, slice(0, TOKEN_TILES))
-            elif i >= 1:
+            elif i == 0:
+                turn(n + 1)
+            else:
                 copy_v(last_b)
-                store(i - 1, slice(2, 4))
+                if i < PAIRS:
+                    store(i - 1, slice(2, 4))
+                else:
+                    store(i - 1, slice(2, 3))
+                    store(i - 1, slice(3, 4))
             if more:
                 for k in range(1, len(banks)):
                     regroup(n, k, "scalar")
-            if n + 2 < OPERANDS:
-                sort_words(n + 2)
             if i < PAIRS:
                 if i > 0:
                     multiply(2 * i)

@@ -18,8 +18,9 @@ K = 2048
 K_PASS = 4 * P
 PASSES = K // K_PASS
 WORDS = K // 2
+AHEAD = 7
 BLOCK = 32
-FIRST_TURNED = 4
+FIRST_TURNED = 5
 HEAD = 128
 HALF = HEAD // 2
 ROWS = 2 * P
@@ -76,7 +77,8 @@ def tile_slidingcacheattention_pa_kernel(
         pair_views = [w[ROWS * n : ROWS * (n + 1), :].rearrange("(b p) k -> p b k", p=P) for (kind, w, out, n) in pairs]
         views = [pair_views[0], x_view[:, 2:4, :]]
         views.extend(pair_views[1:])
-        for view in views:
+        def load_next():
+            view = views[len(rows) - 1]
             loaded = rows_pool.tile([P, 2, K], BF16, name="loaded")
             n = len(rows)
             end = K - K_PASS if n >= FIRST_TURNED else K
@@ -90,6 +92,9 @@ def tile_slidingcacheattention_pa_kernel(
                         out=loaded[BLOCK * q : BLOCK * (q + 1), 1, end:K].rearrange("p (r k) -> p r k", r=4), in_=quarters[q]
                     )
             rows.append(loaded)
+
+        for n in range(AHEAD):
+            load_next()
 
         eps = const.tile([P, 1], F32)
         nc.vector.memset(eps[:], EPS)
@@ -304,13 +309,15 @@ def tile_slidingcacheattention_pa_kernel(
                 make_tables()
 
         for i in range(PAIRS + 1):
-            n = w_tile(i + 1) if i > 0 else 3
+            n = w_tile(i + 1)
             more = n < OPERANDS
             last_a, last_b = 2 * (i - 1), 2 * (i - 1) + 1
             if i == 0:
                 multiply(0)
                 squares(0)
                 norms(0)
+            if len(rows) < OPERANDS:
+                load_next()
             last_rotated = rotated(i - 2) and not rotated(i - 1)
             if last_rotated:
                 result[i - 2] = work.tile([P, 2 * TOKEN_TILES, HEAD], F32, name="result")
@@ -322,7 +329,7 @@ def tile_slidingcacheattention_pa_kernel(
             if last_rotated:
                 add(i - 2, nc.vector, slice(TOKEN_TILES, 2 * TOKEN_TILES))
                 store_head(i - 2, 1)
-            if n + 1 < OPERANDS:
+            if FIRST_TURNED <= n + 1 < OPERANDS:
                 order_words(n + 1)
             if rotated(i - 2) and not last_rotated:
                 begin_result(i - 2)
@@ -338,12 +345,10 @@ def tile_slidingcacheattention_pa_kernel(
             if rotated(i - 1):
                 norms(last_b)
                 products(last_a)
-                if n + 1 < OPERANDS:
+                if FIRST_TURNED <= n + 1 < OPERANDS:
                     turn(n + 1)
                 products(last_b)
-            elif i == 0:
-                turn(n + 1)
-            else:
+            elif i > 0:
                 copy_v(last_b)
                 if i < PAIRS:
                     store(i - 1, slice(2, 4))

@@ -59,17 +59,18 @@ def tile_slidingcacheattention_pa_kernel(
 
         x_view = x[0].rearrange("(p j) k -> p j k", j=TOKEN_TILES)
         rows = [rows_pool.tile([P, 2, K], BF16, name="loaded")]
-        for b in range(2):
-            nc.sync.dma_start(out=rows[0][:, b, :], in_=x_view[:, b, :])
+        def load_quarters(loaded, view):
+            for b in range(2):
+                for half in range(2):
+                    some = slice(K // 2 * half, K // 2 * (half + 1))
+                    nc.sync.dma_start(out=loaded[:, b, some], in_=view[:, b, some])
+
+        load_quarters(rows[0], x_view[:, 0:2, :])
 
         cos = const.tile([P, TOKEN_TILES, HALF], BF16)
         sin = const.tile([P, TOKEN_TILES, HALF], BF16)
         gain_rows = const.tile([P, 2 * HEAD], BF16)
         nc.vector.memset(gain_rows[:], 0.0)
-        nc.sync.dma_start(out=gain_rows[0:1, 0:HEAD], in_=wq_norm.rearrange("(o d) -> o d", o=1))
-        nc.sync.dma_start(out=gain_rows[0:1, HEAD : 2 * HEAD], in_=wk_norm.rearrange("(o d) -> o d", o=1))
-        nc.sync.dma_start(out=cos[:], in_=freqs_cos.rearrange("(p j) i -> p j i", j=TOKEN_TILES))
-        nc.sync.dma_start(out=sin[:], in_=freqs_sin.rearrange("(p j) i -> p j i", j=TOKEN_TILES))
 
         pairs = [("q", Wq, out_0, n) for n in range(Q_PAIRS)]
         pairs.extend([("k", Wk, out_1, n) for n in range(K_PAIRS)])
@@ -81,6 +82,10 @@ def tile_slidingcacheattention_pa_kernel(
             view = views[len(rows) - 1]
             loaded = rows_pool.tile([P, 2, K], BF16, name="loaded")
             n = len(rows)
+            if n < 3:
+                load_quarters(loaded, view)
+                rows.append(loaded)
+                return
             end = K - K_PASS if n >= FIRST_TURNED else K
             nc.sync.dma_start(out=loaded[:, 0, :], in_=view[:, 0, :])
             nc.sync.dma_start(out=loaded[:, 1, :end], in_=view[:, 1, :end])
@@ -95,6 +100,11 @@ def tile_slidingcacheattention_pa_kernel(
 
         for n in range(AHEAD):
             load_next()
+            if len(rows) == 3:
+                nc.sync.dma_start(out=gain_rows[0:1, 0:HEAD], in_=wq_norm.rearrange("(o d) -> o d", o=1))
+                nc.sync.dma_start(out=gain_rows[0:1, HEAD : 2 * HEAD], in_=wk_norm.rearrange("(o d) -> o d", o=1))
+                nc.sync.dma_start(out=cos[:], in_=freqs_cos.rearrange("(p j) i -> p j i", j=TOKEN_TILES))
+                nc.sync.dma_start(out=sin[:], in_=freqs_sin.rearrange("(p j) i -> p j i", j=TOKEN_TILES))
 
         eps = const.tile([P, 1], F32)
         nc.vector.memset(eps[:], EPS)
@@ -111,21 +121,25 @@ def tile_slidingcacheattention_pa_kernel(
 
         tables = {}
 
-        def make_tables():
+        def make_gains():
             gain_psum = acc_psum.tile([P, 2 * HEAD], F32, tag="acc")
             nc.tensor.matmul(out=gain_psum[:], lhsT=ones[:], rhs=gain_rows[:], start=True, stop=True)
             nc.vector.tensor_copy(out=gains[:].rearrange("p n i e -> p (n i e)"), in_=gain_psum[:])
             nc.vector.tensor_copy(out=signed_gains[:, :, :, 0], in_=gains[:, :, :, 0])
             nc.vector.tensor_scalar_mul(out=signed_gains[:, :, :, 1], in0=gains[:, :, :, 1], scalar1=-1.0)
-            for n, kind in enumerate(("q", "k")):
-                tables[kind] = const.tile([P, TOKEN_TILES, 2, HALF, 2], F32, name="table_" + kind)
-                for place, angles, factors in ((0, cos, gains), (1, sin, signed_gains)):
-                    nc.gpsimd.tensor_tensor(
-                        out=tables[kind][:, :, place, :, :],
-                        in0=angles[:].unsqueeze(3).to_broadcast([P, TOKEN_TILES, HALF, 2]),
-                        in1=factors[:, n, :, :].unsqueeze(1).to_broadcast([P, TOKEN_TILES, HALF, 2]),
-                        op=ALU.mult,
-                    )
+
+        def make_table(n, kind):
+            tables[kind] = const.tile([P, TOKEN_TILES, 2, HALF, 2], F32, name="table_" + kind)
+            engine = nc.vector if kind == "q" else nc.gpsimd
+            if kind == "k":
+                nc.vector.memset(tables[kind][:, 0, :, 0, 0:1], 0.0)
+            for place, angles, factors in ((0, cos, gains), (1, sin, signed_gains)):
+                engine.tensor_tensor(
+                    out=tables[kind][:, :, place, :, :],
+                    in0=angles[:].unsqueeze(3).to_broadcast([P, TOKEN_TILES, HALF, 2]),
+                    in1=factors[:, n, :, :].unsqueeze(1).to_broadcast([P, TOKEN_TILES, HALF, 2]),
+                    op=ALU.mult,
+                )
 
         ordered = {}
         turned = {}
@@ -299,14 +313,24 @@ def tile_slidingcacheattention_pa_kernel(
         def rotated(pair):
             return 0 <= pair < PAIRS and pairs[pair][0] != "v"
 
-        for n in range(3):
+        engines = ("scalar", "vector", "scalar", "scalar")
+        flip(0)
+        for k in range(4):
+            regroup(0, k, engines[k])
+        quantise(0, 0)
+        for n in (1, 2):
             flip(n)
-            for k in range(len(banks)):
-                regroup(n, k, "vector" if k == 1 else "scalar")
-            quantise(n, 0)
-            quantise(n, 1)
-            if n == 0:
-                make_tables()
+            regroup(n, 0, engines[0])
+            regroup(n, 1, engines[1])
+            if n == 1:
+                quantise(0, 1)
+            else:
+                quantise(1, 0)
+                quantise(1, 1)
+            regroup(n, 2, engines[2])
+            regroup(n, 3, engines[3])
+        quantise(2, 0)
+        quantise(2, 1)
 
         for i in range(PAIRS + 1):
             n = w_tile(i + 1)
@@ -316,6 +340,8 @@ def tile_slidingcacheattention_pa_kernel(
                 multiply(0)
                 squares(0)
                 norms(0)
+                make_gains()
+                make_table(0, "q")
             if len(rows) < OPERANDS:
                 load_next()
             last_rotated = rotated(i - 2) and not rotated(i - 1)
@@ -344,6 +370,8 @@ def tile_slidingcacheattention_pa_kernel(
                 regroup(n, 0, "scalar")
             if rotated(i - 1):
                 norms(last_b)
+                if i == 1:
+                    make_table(1, "k")
                 products(last_a)
                 if FIRST_TURNED <= n + 1 < OPERANDS:
                     turn(n + 1)

@@ -345,18 +345,16 @@ def tile_slidingcacheattention_pa_kernel(
             if len(rows) < OPERANDS:
                 load_next()
             last_rotated = rotated(i - 2) and not rotated(i - 1)
-            if last_rotated:
-                result[i - 2] = work.tile([P, 2 * TOKEN_TILES, HEAD], F32, name="result")
-                add(i - 2, nc.vector, slice(0, TOKEN_TILES))
-                store_head(i - 2, 0)
             if 1 <= i < PAIRS:
                 quantise(w_tile(i), 0)
                 quantise(w_tile(i), 1)
             if last_rotated:
-                add(i - 2, nc.vector, slice(TOKEN_TILES, 2 * TOKEN_TILES))
-                store_head(i - 2, 1)
-            if FIRST_TURNED <= n + 1 < OPERANDS:
-                order_words(n + 1)
+                result[i - 2] = work.tile([P, 2 * TOKEN_TILES, HEAD], F32, name="result")
+                for head in range(2):
+                    add(i - 2, nc.vector, slice(TOKEN_TILES * head, TOKEN_TILES * (head + 1)))
+                    store_head(i - 2, head)
+            if FIRST_TURNED <= n < OPERANDS:
+                order_words(n)
             if rotated(i - 2) and not last_rotated:
                 begin_result(i - 2)
                 add(i - 2, nc.gpsimd, slice(0, 2 * TOKEN_TILES))
@@ -372,9 +370,9 @@ def tile_slidingcacheattention_pa_kernel(
                 norms(last_b)
                 if i == 1:
                     make_table(1, "k")
+                if FIRST_TURNED <= n < OPERANDS:
+                    turn(n)
                 products(last_a)
-                if FIRST_TURNED <= n + 1 < OPERANDS:
-                    turn(n + 1)
                 products(last_b)
             elif i > 0:
                 copy_v(last_b)

@@ -52,6 +52,7 @@ def tile_slidingcacheattention_pa_kernel(
         stage = stack.enter_context(tc.tile_pool(name="stage", bufs=2))
         w_mx = stack.enter_context(tc.tile_pool(name="w_mx", bufs=3))
         work = stack.enter_context(tc.tile_pool(name="work", bufs=4))
+        result_pool = stack.enter_context(tc.tile_pool(name="result_pool", bufs=8))
         turn_pool = stack.enter_context(tc.tile_pool(name="turn_pool", bufs=3))
         terms_pool = stack.enter_context(tc.tile_pool(name="terms_pool", bufs=2))
         flip_psum = stack.enter_context(tc.psum_pool(name="flip_psum", bufs=4))
@@ -272,7 +273,7 @@ def tile_slidingcacheattention_pa_kernel(
                 )
 
         def begin_result(pair):
-            result[pair] = work.tile([P, 2 * TOKEN_TILES, HEAD], F32, name="result")
+            result[pair] = result_pool.tile([P, 2 * TOKEN_TILES, HEAD], F32, name="result")
             nc.vector.memset(result[pair][:, 0, 0:1], 0.0)
 
         def add(pair, engine, some):
@@ -287,7 +288,7 @@ def tile_slidingcacheattention_pa_kernel(
         def copy_v(slot):
             pair, half = slot // 2, slot % 2
             if half == 0:
-                result[pair] = work.tile([P, 2 * TOKEN_TILES, HEAD], F32, name="result")
+                result[pair] = result_pool.tile([P, 2 * TOKEN_TILES, HEAD], F32, name="result")
             for jj in range(2):
                 out_view = result[pair][:].rearrange("p (h j) d -> p j h d", h=2)[:, 2 * half + jj, :, :]
                 in_view = acc[slot][jj].rearrange("p (h d) -> p h d", h=2)
@@ -349,7 +350,7 @@ def tile_slidingcacheattention_pa_kernel(
                 quantise(w_tile(i), 0)
                 quantise(w_tile(i), 1)
             if last_rotated:
-                result[i - 2] = work.tile([P, 2 * TOKEN_TILES, HEAD], F32, name="result")
+                result[i - 2] = result_pool.tile([P, 2 * TOKEN_TILES, HEAD], F32, name="result")
                 for head in range(2):
                     add(i - 2, nc.vector, slice(TOKEN_TILES * head, TOKEN_TILES * (head + 1)))
                     store_head(i - 2, head)

@@ -60,13 +60,8 @@ def tile_slidingcacheattention_pa_kernel(
 
         x_view = x[0].rearrange("(p j) k -> p j k", j=TOKEN_TILES)
         rows = [rows_pool.tile([P, 2, K], BF16, name="loaded")]
-        def load_quarters(loaded, view):
-            for b in range(2):
-                for half in range(2):
-                    some = slice(K // 2 * half, K // 2 * (half + 1))
-                    nc.sync.dma_start(out=loaded[:, b, some], in_=view[:, b, some])
-
-        load_quarters(rows[0], x_view[:, 0:2, :])
+        for b in range(2):
+            nc.sync.dma_start(out=rows[0][:, b, :], in_=x_view[:, b, :])
 
         cos = const.tile([P, TOKEN_TILES, HALF], BF16)
         sin = const.tile([P, TOKEN_TILES, HALF], BF16)
@@ -83,10 +78,6 @@ def tile_slidingcacheattention_pa_kernel(
             view = views[len(rows) - 1]
             loaded = rows_pool.tile([P, 2, K], BF16, name="loaded")
             n = len(rows)
-            if n < 3:
-                load_quarters(loaded, view)
-                rows.append(loaded)
-                return
             end = K - K_PASS if n >= FIRST_TURNED else K
             nc.sync.dma_start(out=loaded[:, 0, :], in_=view[:, 0, :])
             nc.sync.dma_start(out=loaded[:, 1, :end], in_=view[:, 1, :end])

from contextlib import ExitStack

import concourse.masks as masks
import concourse.mybir as mybir

F32 = mybir.dt.float32
BF16 = mybir.dt.bfloat16
U32 = mybir.dt.uint32
U8 = mybir.dt.uint8
FP8X4 = mybir.dt.float8_e4m3fn_x4
ACT = mybir.ActivationFunctionType
ALU = mybir.AluOpType

P = 128
TOKENS = 512
TOKEN_TILES = TOKENS // P
K = 2048
K_PASS = 4 * P
PASSES = K // K_PASS
WORDS = K // 2
AHEAD = 7
BLOCK = 32
FIRST_TURNED = 5
HEAD = 128
HALF = HEAD // 2
ROWS = 2 * P
EPS = 1e-6

Q_PAIRS, K_PAIRS, V_PAIRS = 8, 2, 2
PAIRS = Q_PAIRS + K_PAIRS + V_PAIRS
OPERANDS = 2 + PAIRS
X_TILES = (0, 2)


def w_tile(pair):
    return 1 if pair == 0 else pair + 2


SLOTS = 2 * PAIRS

FLOPS = 2 * TOKENS * K * HEAD * 2 * PAIRS


def tile_slidingcacheattention_pa_kernel(
    tc, x, freqs_cos, freqs_sin, Wq, Wk, Wv, wq_norm, wk_norm, out_0, out_1, out_2
):
    nc = tc.nc
    with ExitStack() as stack:
        stack.enter_context(tc.manual_schedule())
        const = stack.enter_context(tc.tile_pool(name="const", bufs=1))
        rows_pool = stack.enter_context(tc.tile_pool(name="rows", bufs=OPERANDS))
        stage = stack.enter_context(tc.tile_pool(name="stage", bufs=2))
        w_mx = stack.enter_context(tc.tile_pool(name="w_mx", bufs=3))
        work = stack.enter_context(tc.tile_pool(name="work", bufs=4))
        result_pool = stack.enter_context(tc.tile_pool(name="result_pool", bufs=8))
        turn_pool = stack.enter_context(tc.tile_pool(name="turn_pool", bufs=3))
        terms_pool = stack.enter_context(tc.tile_pool(name="terms_pool", bufs=2))
        flip_psum = stack.enter_context(tc.psum_pool(name="flip_psum", bufs=4))
        acc_psum = stack.enter_context(tc.psum_pool(name="acc_psum", bufs=4))

        x_view = x[0].rearrange("(p j) k -> p j k", j=TOKEN_TILES)
        rows = [rows_pool.tile([P, 2, K], BF16, name="loaded")]
        for b in range(2):
            nc.sync.dma_start(out=rows[0][:, b, :], in_=x_view[:, b, :])

        cos = const.tile([P, TOKEN_TILES, HALF], BF16)
        sin = const.tile([P, TOKEN_TILES, HALF], BF16)
        gain_rows = const.tile([P, 2 * HEAD], BF16)
        nc.vector.memset(gain_rows[:], 0.0)

        pairs = [("q", Wq, out_0, n) for n in range(Q_PAIRS)]
        pairs.extend([("k", Wk, out_1, n) for n in range(K_PAIRS)])
        pairs.extend([("v", Wv, out_2, n) for n in range(V_PAIRS)])
        pair_views = [w[ROWS * n : ROWS * (n + 1), :].rearrange("(b p) k -> p b k", p=P) for (kind, w, out, n) in pairs]
        views = [pair_views[0], x_view[:, 2:4, :]]
        views.extend(pair_views[1:])
        def load_next():
            view = views[len(rows) - 1]
            loaded = rows_pool.tile([P, 2, K], BF16, name="loaded")
            n = len(rows)
            end = K - K_PASS if n >= FIRST_TURNED else K
            nc.sync.dma_start(out=loaded[:, 0, :], in_=view[:, 0, :])
            nc.sync.dma_start(out=loaded[:, 1, :end], in_=view[:, 1, :end])
            if end < K:
                kind, w, out, m = pairs[n - 2 if n > 2 else 0]
                quarters = w[ROWS * m + P : ROWS * (m + 1), end:K].rearrange("(r i) (q k) -> q i r k", i=BLOCK, q=4)
                for q in range(4):
                    nc.sync.dma_start(
                        out=loaded[BLOCK * q : BLOCK * (q + 1), 1, end:K].rearrange("p (r k) -> p r k", r=4), in_=quarters[q]
                    )
            rows.append(loaded)

        for n in range(AHEAD):
            load_next()
            if len(rows) == 3:
                nc.sync.dma_start(out=gain_rows[0:1, 0:HEAD], in_=wq_norm.rearrange("(o d) -> o d", o=1))
                nc.sync.dma_start(out=gain_rows[0:1, HEAD : 2 * HEAD], in_=wk_norm.rearrange("(o d) -> o d", o=1))
                nc.sync.dma_start(out=cos[:], in_=freqs_cos.rearrange("(p j) i -> p j i", j=TOKEN_TILES))
                nc.sync.dma_start(out=sin[:], in_=freqs_sin.rearrange("(p j) i -> p j i", j=TOKEN_TILES))

        eps = const.tile([P, 1], F32)
        nc.vector.memset(eps[:], EPS)
        warm = const.tile([P, 1], F32)
        nc.scalar.activation(out=warm[:], in_=eps[:], func=ACT.Abs_reciprocal_sqrt)

        ident = const.tile([P, P], F32)
        masks.make_identity(nc, ident[:])

        ones = const.tile([P, P], BF16)
        nc.vector.memset(ones[:], 1.0)
        gains = const.tile([P, 2, HALF, 2], F32)
        signed_gains = const.tile([P, 2, HALF, 2], F32)

        tables = {}

        def make_gains():
            gain_psum = acc_psum.tile([P, 2 * HEAD], F32, tag="acc")
            nc.tensor.matmul(out=gain_psum[:], lhsT=ones[:], rhs=gain_rows[:], start=True, stop=True)
            nc.vector.tensor_copy(out=gains[:].rearrange("p n i e -> p (n i e)"), in_=gain_psum[:])
            nc.vector.tensor_copy(out=signed_gains[:, :, :, 0], in_=gains[:, :, :, 0])
            nc.vector.tensor_scalar_mul(out=signed_gains[:, :, :, 1], in0=gains[:, :, :, 1], scalar1=-1.0)

        def make_table(n, kind):
            tables[kind] = const.tile([P, TOKEN_TILES, 2, HALF, 2], F32, name="table_" + kind)
            engine = nc.vector if kind == "q" else nc.gpsimd
            if kind == "k":
                nc.vector.memset(tables[kind][:, 0, :, 0, 0:1], 0.0)
            for place, angles, factors in ((0, cos, gains), (1, sin, signed_gains)):
                engine.tensor_tensor(
                    out=tables[kind][:, :, place, :, :],
                    in0=angles[:].unsqueeze(3).to_broadcast([P, TOKEN_TILES, HALF, 2]),
                    in1=factors[:, n, :, :].unsqueeze(1).to_broadcast([P, TOKEN_TILES, HALF, 2]),
                    op=ALU.mult,
                )

        ordered = {}
        turned = {}
        flipped = {}
        grouped = {}
        codes = {}
        scales = {}
        acc = {}
        sumsq = {}
        inv_rms = {}
        terms = {}
        result = {}

        banks = [(0, 0), (0, 2), (1, 0), (1, 2)]

        def flip(n):
            flipped[n] = []
            for b, first in banks:
                bank = flip_psum.tile([P, 2, 2, P], F32, name="flipped")
                for g in range(2):
                    if n >= FIRST_TURNED and b == 1 and first + g == PASSES - 1:
                        continue
                    for u in range(2):
                        word = 2 * P * (first + g)
                        words = rows[n][:, b, :].bitcast(F32)[:, word + u : word + 2 * P : 2]
                        nc.tensor.transpose(bank[:, g, u, :], words, ident[:])
                flipped[n].append(bank)

        def order_words(n):
            ordered[n] = turn_pool.tile([P, 4, 2, BLOCK], F32, name="ordered", align_bytes=64)
            raw = rows[n][:, 1, K - K_PASS : K].bitcast(F32)
            nc.vector.tensor_copy(out=ordered[n][:], in_=raw.rearrange("p (r j u) -> p r u j", r=4, u=2))

        def turn(n):
            turned[n] = turn_pool.tile([P, 4, 2, BLOCK], F32, name="turned", align_bytes=64)
            nc.vector.transpose(
                out=turned[n][:].rearrange("p r u i -> p (r u i)"), in_=ordered[n][:].rearrange("p r u j -> p (r u j)")
            )

        def regroup(n, k, engine):
            if k == 0:
                grouped[n] = stage.tile([P, PASSES, ROWS, 4], BF16, name="grouped", align_bytes=64)
            b, first = banks[k]
            if n >= FIRST_TURNED and k == 3:
                out_words = grouped[n][:, first, P:, :].rearrange("p r t -> p (r t)").bitcast(F32)
                nc.scalar.copy(
                    out=out_words.rearrange("p (r u) -> p r u", u=2), in_=flipped[n][k][:, 0, :, :].rearrange("p u r -> p r u")
                )
                out_words = grouped[n][:, first + 1, P:, :].rearrange("p r t -> p (r t)").bitcast(F32)
                nc.scalar.copy(
                    out=out_words.rearrange("p (r i u) -> p r i u", r=4, u=2), in_=turned[n][:].rearrange("p r u i -> p r i u")
                )
                return
            out_rows = grouped[n][:, first : first + 2, P * b : P * (b + 1), :]
            out_words = out_rows.rearrange("p g r t -> p g (r t)").bitcast(F32).rearrange("p g (r u) -> p g r u", u=2)
            in_words = flipped[n][k][:].rearrange("p g u r -> p g r u")
            if engine == "scalar":
                nc.scalar.copy(out=out_words, in_=in_words)
            else:
                nc.vector.tensor_copy(out=out_words, in_=in_words)

        def quantise(n, half):
            if half == 0:
                pool, name = (const, "x%d" % n) if n in X_TILES else (w_mx, "w")
                codes[n] = pool.tile([P, PASSES, ROWS], U32, name=name + "_codes", align_bytes=64)
                scales[n] = pool.tile([P, PASSES, ROWS], U8, name=name + "_scales", align_bytes=64)
            two_passes = slice(2 * half, 2 * half + 2)
            nc.vector.quantize_mx(
                out=codes[n][:, two_passes, :].rearrange("p g r -> p (g r)").bitcast(FP8X4),
                scales=scales[n][:, two_passes, :].rearrange("p g r -> p (g r)"),
                in_=grouped[n][:, two_passes, :, :].rearrange("p g r t -> p (g r t)"),
            )

        def multiply(slot):
            xt, wt = X_TILES[slot % 2], w_tile(slot // 2)
            if slot < SLOTS - 1:
                bank = acc_psum.tile([P, 2, 2 * HEAD], F32, name="acc")
                acc[slot] = [bank[:, jj, :] for jj in range(2)]
            else:
                acc[slot] = []
                for jj in range(2):
                    bank = flip_psum.tile([P, 2 * HEAD], F32, tag="flipped")
                    acc[slot].append(bank[:])
            for jj in range(2):
                tok = slice(P * jj, P * (jj + 1))
                for g in range(PASSES):
                    nc.tensor.matmul_mx(
                        out=acc[slot][jj],
                        lhsT=codes[xt][:, g, tok].bitcast(FP8X4),
                        lhsT_scale=scales[xt][:, g, tok],
                        rhs=codes[wt][:, g, :].bitcast(FP8X4),
                        rhs_scale=scales[wt][:, g, :],
                        start=(g == 0),
                        stop=(g == PASSES - 1),
                    )

        def segments(slot):
            half = slot % 2
            return [
                (2 * jj + hh, 2 * half + jj, acc[slot][jj][:, HEAD * hh : HEAD * (hh + 1)])
                for jj in range(2)
                for hh in range(2)
            ]

        def squares(slot):
            sumsq[slot] = work.tile([P, 4], F32, name="sumsq")
            for s, tile, segment in segments(slot):
                scratch = work.tile([P, HEAD], F32, name="scratch")
                nc.scalar.activation(out=scratch[:], in_=segment, func=ACT.Square, accum_out=sumsq[slot][:, s : s + 1])

        def norms(slot):
            inv_rms[slot] = work.tile([P, 4], F32, name="inv_rms")
            nc.scalar.activation(
                out=inv_rms[slot][:], in_=sumsq[slot][:], func=ACT.Abs_reciprocal_sqrt, bias=eps[:], scale=1.0 / HEAD
            )

        def products(slot):
            pair = slot // 2
            if slot % 2 == 0:
                terms[pair] = terms_pool.tile([P, 2 * TOKEN_TILES, 2, HEAD], F32, name="terms")
            table = tables[pairs[pair][0]]
            for s, tile, segment in segments(slot):
                nc.vector.scalar_tensor_tensor(
                    out=terms[pair][:, TOKEN_TILES * (s % 2) + tile, :, :],
                    in0=segment.unsqueeze(1).to_broadcast([P, 2, HEAD]),
                    scalar=inv_rms[slot][:, s : s + 1],
                    in1=table[:, tile, :, :, :].rearrange("p v i e -> p v (i e)"),
                    op0=ALU.mult,
                    op1=ALU.mult,
                )

        def begin_result(pair):
            result[pair] = result_pool.tile([P, 2 * TOKEN_TILES, HEAD], F32, name="result")
            nc.vector.memset(result[pair][:, 0, 0:1], 0.0)

        def add(pair, engine, some):
            own, other = [terms[pair][:, some, v, :].rearrange("p r (i e) -> p r i e", e=2) for v in range(2)]
            engine.tensor_tensor(
                out=result[pair][:, some, :].rearrange("p r (i e) -> p r i e", e=2),
                in0=own,
                in1=other[:, :, :, ::-1],
                op=ALU.add,
            )

        def copy_v(slot):
            pair, half = slot // 2, slot % 2
            if half == 0:
                result[pair] = result_pool.tile([P, 2 * TOKEN_TILES, HEAD], F32, name="result")
            for jj in range(2):
                out_view = result[pair][:].rearrange("p (h j) d -> p j h d", h=2)[:, 2 * half + jj, :, :]
                in_view = acc[slot][jj].rearrange("p (h d) -> p h d", h=2)
                if half == 0 or (slot == SLOTS - 1 and jj == 0):
                    nc.scalar.copy(out=out_view, in_=in_view)
                else:
                    nc.vector.tensor_copy(out=out_view, in_=in_view)

        def store(pair, tiles):
            kind, w, out, n = pairs[pair]
            nc.sync.dma_start(
                out=out[0, 2 * n : 2 * n + 2].rearrange("h (p j) d -> p h j d", j=TOKEN_TILES)[:, :, tiles, :],
                in_=result[pair][:].rearrange("p (h j) d -> p h j d", h=2)[:, :, tiles, :],
            )

        def store_head(pair, h):
            kind, w, out, n = pairs[pair]
            nc.sync.dma_start(
                out=out[0, 2 * n + h].rearrange("(p j) d -> p j d", j=TOKEN_TILES),
                in_=result[pair][:, TOKEN_TILES * h : TOKEN_TILES * (h + 1), :],
            )

        def rotated(pair):
            return 0 <= pair < PAIRS and pairs[pair][0] != "v"

        engines = ("scalar", "vector", "scalar", "scalar")
        flip(0)
        for k in range(4):
            regroup(0, k, engines[k])
        quantise(0, 0)
        for n in (1, 2):
            flip(n)
            regroup(n, 0, engines[0])
            regroup(n, 1, engines[1])
            if n == 1:
                quantise(0, 1)
            else:
                quantise(1, 0)
                quantise(1, 1)
            regroup(n, 2, engines[2])
            regroup(n, 3, engines[3])
        quantise(2, 0)
        quantise(2, 1)

        for i in range(PAIRS + 1):
            n = w_tile(i + 1)
            more = n < OPERANDS
            last_a, last_b = 2 * (i - 1), 2 * (i - 1) + 1
            if i == 0:
                multiply(0)
                squares(0)
                norms(0)
                make_gains()
                make_table(0, "q")
            if len(rows) < OPERANDS:
                load_next()
            last_rotated = rotated(i - 2) and not rotated(i - 1)
            if 1 <= i < PAIRS:
                quantise(w_tile(i), 0)
                quantise(w_tile(i), 1)
            if last_rotated:
                result[i - 2] = result_pool.tile([P, 2 * TOKEN_TILES, HEAD], F32, name="result")
                for head in range(2):
                    add(i - 2, nc.vector, slice(TOKEN_TILES * head, TOKEN_TILES * (head + 1)))
                    store_head(i - 2, head)
            if FIRST_TURNED <= n < OPERANDS:
                order_words(n)
            if rotated(i - 2) and not last_rotated:
                begin_result(i - 2)
                add(i - 2, nc.gpsimd, slice(0, 2 * TOKEN_TILES))
                store_head(i - 2, 0)
                store_head(i - 2, 1)
            if more:
                flip(n)
            if rotated(i - 1):
                squares(last_b)
            if more:
                regroup(n, 0, "scalar")
            if rotated(i - 1):
                norms(last_b)
                if i == 1:
                    make_table(1, "k")
                if FIRST_TURNED <= n < OPERANDS:
                    turn(n)
                products(last_a)
                products(last_b)
            elif i > 0:
                copy_v(last_b)
                if i < PAIRS:
                    store(i - 1, slice(2, 4))
                else:
                    store(i - 1, slice(2, 3))
                    store(i - 1, slice(3, 4))
            if more:
                for k in range(1, len(banks)):
                    regroup(n, k, "scalar")
            if i < PAIRS:
                if i > 0:
                    multiply(2 * i)
                    if rotated(i):
                        squares(2 * i)
                        norms(2 * i)
                    else:
                        copy_v(2 * i)
                        store(i, slice(0, 2))
                multiply(2 * i + 1)
